import numpy as np
import ml_dtypes


def mxq(x, axis, fmt="e4m3"):
    dtype, down = {"e4m3": (ml_dtypes.float8_e4m3fn, 7), "e5m2": (ml_dtypes.float8_e5m2, 14)}[fmt]
    v = np.moveaxis(np.asarray(x, np.float32).astype(ml_dtypes.bfloat16).astype(np.float64), axis, -1)
    blocks = v.reshape(v.shape[:-1] + (-1, 32))
    amax = np.abs(blocks).max(-1, keepdims=True)
    byte = np.maximum(np.where(amax > 0, np.frexp(amax)[1] - 1 + 127, 0) - down, 1)
    scale = np.exp2(byte - 127.0)
    codes = (blocks / scale).astype(np.float32).astype(dtype).astype(np.float64)
    return np.moveaxis((codes * scale).reshape(v.shape), -1, axis)


WIDE = False


def mx_kscale(k):
    if not WIDE:
        return np.ones(k)
    levels = np.array([10, -10, 5, -5, 0])
    if k % 512:
        return np.exp2(np.random.permutation(np.resize(levels, k // 32))).repeat(32)
    a = np.empty((k // 512, 16))
    for p in range(k // 512):
        a[p, :8] = np.random.permutation(np.resize(levels, 8))
        for g in range(8):
            far = levels[np.abs(levels - a[p, g]) >= 10]
            a[p, g + 8] = far[np.random.randint(len(far))]
    return np.exp2(a.ravel()).repeat(32)


BF16 = ml_dtypes.bfloat16


def bf(x):
    return np.asarray(x, np.float32).astype(BF16)


def f64(x):
    return np.asarray(x).astype(np.float64)


H, L, B, S = 1024, 2, 128, 32


def sigmoid(v):
    return 1.0 / (1.0 + np.exp(-v))


def setup_inputs():
    r = np.random.standard_normal
    s, t, u = mx_kscale(H), mx_kscale(H), mx_kscale(H)
    st = np.concatenate([s, t])
    return {
        "x": bf(r((B, H)) * s),
        "enc_seq": bf(r((S, B, H)) * t),
        "attn_W": bf(r((H, H)) / np.sqrt(H) / s[None, :] / t[:, None]),
        "attn_b": bf(r(H) * 0.5 / t),
        "h_prev": bf(r((B, H)) * u),
        "c_prev": bf(r((B, H))),
        "W_ih0": bf(r((4 * H, H + H)) * 0.6 / np.sqrt(H) / st[None, :]),
        "W_hh0": bf(r((4 * H, H)) * 0.6 / np.sqrt(H) / u[None, :]),
        "b_ih0": bf(r(4 * H) * 0.3),
        "b_hh0": bf(r(4 * H) * 0.3),
    }


def reference(x, enc_seq, attn_W, attn_b, h_prev, c_prev, W_ih0, W_hh0, b_ih0, b_hh0):
    enc = f64(enc_seq)
    xq = mxq(f64(x), 1, "e4m3")
    attn_lin = (xq @ mxq(f64(attn_W).T, 0, "e4m3")) + f64(attn_b)
    scores = attn_lin[None, :, :] * enc
    e = np.exp(scores - scores.max(0, keepdims=True))
    w = e / e.sum(0, keepdims=True)
    attention = (enc * w).sum(0)
    aq = mxq(attention, 1, "e4m3")
    w_x = mxq(f64(W_ih0)[:, :H].T, 0, "e4m3")
    w_a = mxq(f64(W_ih0)[:, H:].T, 0, "e4m3")
    hq = mxq(f64(h_prev), 1, "e4m3")
    gates = (xq @ w_x) + (aq @ w_a) + f64(b_ih0) + (hq @ mxq(f64(W_hh0).T, 0, "e4m3")) + f64(b_hh0)
    i, f, g, o = np.split(gates, 4, axis=-1)
    c_new = sigmoid(f) * f64(c_prev) + sigmoid(i) * np.tanh(g)
    h_new = sigmoid(o) * np.tanh(c_new)
    return h_new, c_new

@@ -1,0 +1,364 @@
+from contextlib import ExitStack
+
+import concourse.mybir as mybir
+from concourse.masks import make_identity
+
+F32 = mybir.dt.float32
+BF16 = mybir.dt.bfloat16
+I32 = mybir.dt.int32
+U32 = mybir.dt.uint32
+U8 = mybir.dt.uint8
+FP8X4 = mybir.dt.float8_e4m3fn_x4
+ALU = mybir.AluOpType
+ACT = mybir.ActivationFunctionType
+
+P = 128
+H = 1024
+S = 32
+K_PASS = 512
+PASS_WORDS = K_PASS // 2
+H_PASSES = H // K_PASS
+N_BLOCK = 512
+ROW_TILES = N_BLOCK // P
+H_BLOCKS = H // N_BLOCK
+GATE_BLOCKS = 4 * H_BLOCKS
+ROUNDS = 4
+PEAK_FEATS = K_PASS // 2
+SCALAR_PART = P // 2
+QUARTER = S // 4
+S_HALF = S // 2
+HALVES = S // S_HALF
+
+FLOPS = 2 * P * (H * H + 4 * H * 3 * H)
+
+
+def load_weight_rows(nc, stage, rows):
+    w_rows = stage.tile([P, ROW_TILES, H], BF16, tag="w_rows", bufs=3)
+    nc.sync.dma_start(out=w_rows[:], in_=rows.rearrange("(t p) k -> p t k", p=P))
+    return w_rows[:].bitcast(F32)
+
+
+def quantise_weight_pass(nc, psum, stage, ident, words, codes, plane):
+    grouped = stage.tile([P, 4 * N_BLOCK], BF16, tag="grouped", bufs=3, align_bytes=64)
+    grouped_words = grouped[:].bitcast(F32).rearrange("p (r u) -> p r u", u=2)
+    for pair in range(ROW_TILES // 2):
+        bank = psum.tile([P, 2, 2 * P], F32, tag="wt", bufs=3)
+        for i in range(2):
+            for u in range(2):
+                nc.tensor.transpose(
+                    bank[:, u, i * P : (i + 1) * P],
+                    words[:, 2 * pair + i, u : PASS_WORDS : 2],
+                    ident[:],
+                )
+        nc.scalar.copy(
+            out=grouped_words[:, pair * 2 * P : (pair + 1) * 2 * P, :],
+            in_=bank[:].rearrange("p u r -> p r u"),
+        )
+    nc.vector.quantize_mx(out=codes.bitcast(FP8X4), scales=plane, in_=grouped[:])
+
+
+def quantise_activations(nc, psum, stage, ident, rows, codes, planes):
+    words = rows[:].bitcast(F32)
+    bank = psum.tile([P, 2 * H_PASSES, P], F32, tag="wt", bufs=3)
+    for q in range(2 * H_PASSES):
+        nc.tensor.transpose(bank[:, q, :], words[:, (q // 2) * PASS_WORDS + q % 2 : (q // 2 + 1) * PASS_WORDS : 2], ident[:])
+    grouped = stage.tile([P, 4 * H_PASSES * P], BF16, tag="act_grouped", bufs=1, align_bytes=64)
+    nc.scalar.copy(
+        out=grouped[:].bitcast(F32).rearrange("p (g b u) -> p g b u", g=H_PASSES, u=2),
+        in_=bank[:].rearrange("p (g u) b -> p g b u", u=2),
+    )
+    nc.vector.quantize_mx(
+        out=codes[:].rearrange("p g b -> p (g b)").bitcast(FP8X4),
+        scales=planes[:].rearrange("p g b -> p (g b)"),
+        in_=grouped[:],
+    )
+
+
+def multiply_passes(nc, psum, stage, ident, acc, operands):
+    passes = []
+    for w_words, act_codes, act_planes in operands:
+        for g in range(H_PASSES):
+            w_codes = stage.tile([P, N_BLOCK], U32, tag="w_codes", bufs=4, align_bytes=64)
+            w_plane = stage.tile([P, N_BLOCK], U8, tag="w_plane", bufs=4, align_bytes=64)
+            quantise_weight_pass(
+                nc, psum, stage, ident,
+                w_words[:, :, g * PASS_WORDS : (g + 1) * PASS_WORDS], w_codes[:], w_plane[:],
+            )
+            passes.append((act_codes[:, g, :], act_planes[:, g, :], w_codes, w_plane))
+    for i, (a_codes, a_plane, w_codes, w_plane) in enumerate(passes):
+        nc.tensor.matmul_mx(
+            out=acc[:],
+            lhsT=a_codes.bitcast(FP8X4),
+            lhsT_scale=a_plane,
+            rhs=w_codes[:].bitcast(FP8X4),
+            rhs_scale=w_plane[:],
+            start=(i == 0),
+            stop=(i == len(passes) - 1),
+        )
+
+
+def tile_decoderlstm_pa_kernel(
+    tc, x, enc_seq, attn_W, attn_b, h_prev, c_prev, W_ih0, W_hh0, b_ih0, b_hh0, out_0, out_1
+):
+    nc = tc.nc
+    with ExitStack() as stack:
+        const = stack.enter_context(tc.tile_pool(name="const", bufs=1))
+        keep = stack.enter_context(tc.tile_pool(name="keep", bufs=1))
+        stage = stack.enter_context(tc.tile_pool(name="stage", bufs=2))
+        work = stack.enter_context(tc.tile_pool(name="work", bufs=2))
+        psum = stack.enter_context(tc.psum_pool(name="psum", bufs=2))
+
+        def load_enc_pass(g):
+            enc = work.tile([P, S, K_PASS], BF16, tag="enc")
+            feats = slice(g * K_PASS, (g + 1) * K_PASS)
+            for i in range(S // QUARTER):
+                steps = slice(i * QUARTER, (i + 1) * QUARTER)
+                nc.sync.dma_start(out=enc[:, steps, :], in_=enc_seq[steps, :, feats].rearrange("s b j -> b s j"))
+            return enc
+
+        ident = const.tile([P, P], F32)
+        make_identity(nc, ident[:])
+        ones = const.tile([P, P], BF16)
+        nc.vector.memset(ones[:], 1.0)
+
+        enc_passes = [load_enc_pass(0)]
+        x_sb = stage.tile([P, H], BF16, tag="w_rows", bufs=3)
+        nc.sync.dma_start(out=x_sb[:], in_=x)
+        attn_w_words = [
+            load_weight_rows(nc, stage, attn_W[nb * N_BLOCK : (nb + 1) * N_BLOCK, :]) for nb in range(H_BLOCKS)
+        ]
+        bias_rows = work.tile([P, 4 * H], BF16, tag="half_s", bufs=2)
+        attn_b_rows = work.tile([P, H], BF16, tag="half_v", bufs=3)
+        nc.vector.memset(bias_rows[:].bitcast(I32), 0)
+        nc.vector.memset(attn_b_rows[:].bitcast(I32), 0)
+        nc.sync.dma_start(out=attn_b_rows[0:1, :], in_=attn_b.rearrange("(o n) -> o n", o=1))
+        nc.sync.dma_start(out=bias_rows[0:1, 0 : 4 * H], in_=b_ih0.rearrange("(o n) -> o n", o=1))
+        nc.sync.dma_start(out=bias_rows[1:2, 0 : 4 * H], in_=b_hh0.rearrange("(o n) -> o n", o=1))
+        h_sb = stage.tile([P, H], BF16, tag="act_rows", bufs=1)
+        nc.sync.dma_start(out=h_sb[:], in_=h_prev)
+        c_sb = keep.tile([P, H], BF16)
+        nc.sync.dma_start(out=c_sb[:], in_=c_prev)
+
+        x_codes = keep.tile([P, H_PASSES, P], U32, align_bytes=64)
+        x_planes = keep.tile([P, H_PASSES, P], U8, align_bytes=64)
+        quantise_activations(nc, psum, stage, ident, x_sb, x_codes, x_planes)
+        h_codes = keep.tile([P, H_PASSES, P], U32, align_bytes=64)
+        h_planes = keep.tile([P, H_PASSES, P], U8, align_bytes=64)
+        quantise_activations(nc, psum, stage, ident, h_sb, h_codes, h_planes)
+
+        attn_lin = keep.tile([P, H], F32)
+        for nb in range(H_BLOCKS):
+            cols = slice(nb * N_BLOCK, (nb + 1) * N_BLOCK)
+            spread = psum.tile([P, N_BLOCK], F32, tag="acc")
+            nc.tensor.matmul(
+                out=spread[:], lhsT=ones[:], rhs=attn_b_rows[:, cols],
+                start=True, stop=True,
+            )
+            nc.scalar.copy(out=attn_lin[:, cols], in_=spread[:])
+            acc = psum.tile([P, N_BLOCK], F32, tag="acc")
+            multiply_passes(nc, psum, stage, ident, acc, [(attn_w_words[nb], x_codes, x_planes)])
+            nc.vector.tensor_tensor(out=attn_lin[:, cols], in0=acc[:], in1=attn_lin[:, cols], op=ALU.add)
+
+        gates_xh = keep.tile([P, 4 * H], F32)
+        for nb in range(GATE_BLOCKS):
+            cols = slice(nb * N_BLOCK, (nb + 1) * N_BLOCK)
+            spread = psum.tile([P, N_BLOCK], F32, tag="acc")
+            nc.tensor.matmul(out=spread[:], lhsT=ones[:], rhs=bias_rows[:, cols], start=True, stop=True)
+            nc.scalar.copy(out=gates_xh[:, cols], in_=spread[:])
+
+        wa_codes = keep.tile([P, GATE_BLOCKS, H_PASSES, N_BLOCK], U32, align_bytes=64)
+        wa_planes = keep.tile([P, GATE_BLOCKS // 2, N_BLOCK], U8, align_bytes=64)
+
+        def wa_plane(nb, g):
+            row = 4 * (2 * (nb % 2) + g)
+            return wa_planes[row:P, nb // 2, :]
+
+        att_codes = keep.tile([P, H_PASSES, P], U32, align_bytes=64)
+        att_planes = keep.tile([P, H_PASSES, P], U8, align_bytes=64)
+
+        def gate_block(nb):
+            rows = slice(nb * N_BLOCK, (nb + 1) * N_BLOCK)
+            wx_words = load_weight_rows(nc, stage, W_ih0[rows, 0:H])
+            wh_words = load_weight_rows(nc, stage, W_hh0[rows, :])
+            wa_words = load_weight_rows(nc, stage, W_ih0[rows, H : 2 * H])
+            acc = psum.tile([P, N_BLOCK], F32, tag="acc")
+            multiply_passes(
+                nc, psum, stage, ident, acc, [(wx_words, x_codes, x_planes), (wh_words, h_codes, h_planes)]
+            )
+            nc.vector.tensor_tensor(out=gates_xh[:, rows], in0=acc[:], in1=gates_xh[:, rows], op=ALU.add)
+            for g in range(H_PASSES):
+                quantise_weight_pass(
+                    nc, psum, stage, ident,
+                    wa_words[:, :, g * PASS_WORDS : (g + 1) * PASS_WORDS],
+                    wa_codes[:, nb, g, :], wa_plane(nb, g),
+                )
+
+        def negated_peaks(g, part, neg_peak):
+            here = slice(part * PEAK_FEATS, (part + 1) * PEAK_FEATS)
+            enc = enc_passes[g][:, :, here]
+            feats = slice(g * K_PASS + part * PEAK_FEATS, g * K_PASS + (part + 1) * PEAK_FEATS)
+            top = work.tile([P, QUARTER, PEAK_FEATS], BF16, tag="top", bufs=1)
+            low = work.tile([P, QUARTER, PEAK_FEATS], BF16, tag="low", bufs=1)
+            nc.vector.tensor_tensor(out=top[:], in0=enc[:, 0:QUARTER, :], in1=enc[:, QUARTER : 2 * QUARTER, :], op=ALU.max)
+            nc.vector.tensor_tensor(out=low[:], in0=enc[:, 0:QUARTER, :], in1=enc[:, QUARTER : 2 * QUARTER, :], op=ALU.min)
+            for i in range(2, S // QUARTER):
+                steps = slice(i * QUARTER, (i + 1) * QUARTER)
+                nc.vector.tensor_tensor(out=top[:], in0=top[:], in1=enc[:, steps, :], op=ALU.max)
+                nc.vector.tensor_tensor(out=low[:], in0=low[:], in1=enc[:, steps, :], op=ALU.min)
+            half = QUARTER // 2
+            while half >= 1:
+                nc.vector.tensor_tensor(out=top[:, 0:half, :], in0=top[:, 0:half, :], in1=top[:, half : 2 * half, :], op=ALU.max)
+                nc.vector.tensor_tensor(out=low[:, 0:half, :], in0=low[:, 0:half, :], in1=low[:, half : 2 * half, :], op=ALU.min)
+                half //= 2
+            neg_top = work.tile([P, PEAK_FEATS], F32, tag="neg_top", bufs=1)
+            neg_low = work.tile([P, PEAK_FEATS], F32, tag="neg_low", bufs=1)
+            nc.vector.scalar_tensor_tensor(
+                out=neg_top[:], in0=attn_lin[:, feats], scalar=-1.0, in1=top[:, 0, :], op0=ALU.mult, op1=ALU.mult
+            )
+            nc.vector.scalar_tensor_tensor(
+                out=neg_low[:], in0=attn_lin[:, feats], scalar=-1.0, in1=low[:, 0, :], op0=ALU.mult, op1=ALU.mult
+            )
+            nc.vector.tensor_tensor(out=neg_peak[:, here], in0=neg_top[:], in1=neg_low[:], op=ALU.min)
+
+        def chunk_of(g, t):
+            return enc_passes[g][:].rearrange("b s (p t) -> b s t p", t=4)[:, :, t, :]
+
+        def sum_over_s(total, tiles, part):
+            for i in range(S_HALF):
+                s = part * S_HALF + i
+                nc.tensor.matmul(
+                    out=total[:], lhsT=tiles[:, i, :], rhs=ident[:], is_transpose=True,
+                    start=(s == 0), stop=(s == S - 1),
+                )
+
+        def attention_by_scalar(g, t, neg_peak, mean):
+            enc = enc_passes[g]
+            enc_c = chunk_of(g, t)
+            exp_sum = work.tile([P, P], F32, tag="exp_sum")
+            exps = []
+            for half in range(P // SCALAR_PART):
+                exps_h = work.tile([P, SCALAR_PART, S], F32, tag="half_s", bufs=2)
+                for i in range(SCALAR_PART):
+                    p = half * SCALAR_PART + i
+                    j = 4 * p + t
+                    nc.scalar.activation(
+                        out=exps_h[:, i, :],
+                        in_=enc[:, :, j],
+                        func=ACT.Exp,
+                        scale=attn_lin[:, g * K_PASS + j : g * K_PASS + j + 1],
+                        bias=neg_peak[:, j : j + 1],
+                        accum_out=exp_sum[:, p : p + 1],
+                    )
+                exps.append(exps_h)
+            exp_total = psum.tile([P, P], F32, tag="sums", bufs=3)
+            nc.tensor.transpose(exp_total[:], exp_sum[:], ident[:])
+            inverse = work.tile([P, P], F32, tag="inverse")
+            nc.vector.reciprocal(out=inverse[:], in_=exp_total[:])
+            total = psum.tile([P, P], F32, tag="sums", bufs=3)
+            for part in range(HALVES):
+                steps = slice(part * S_HALF, (part + 1) * S_HALF)
+                terms = work.tile([P, S_HALF, P], F32, tag="half_v", bufs=3)
+                for half in range(P // SCALAR_PART):
+                    cols = slice(half * SCALAR_PART, (half + 1) * SCALAR_PART)
+                    nc.vector.tensor_tensor(
+                        out=terms[:, :, cols].rearrange("b (h l) p -> b h p l", l=2),
+                        in0=exps[half][:, :, steps].rearrange("b p (h l) -> b h p l", l=2),
+                        in1=enc_c[:, steps, cols].rearrange("b (h l) p -> b h p l", l=2),
+                        op=ALU.mult,
+                    )
+                sum_over_s(total, terms, part)
+            nc.vector.tensor_tensor(out=mean, in0=total[:], in1=inverse[:], op=ALU.mult)
+            return inverse
+
+        def attention_by_vector(g, t, neg_peak, mean):
+            enc_c = chunk_of(g, t)
+            lin_c = attn_lin[:, g * K_PASS : (g + 1) * K_PASS].rearrange("b (p t) -> b t p", t=4)[:, t, :]
+            neg_peak_c = neg_peak[:].rearrange("b (p t) -> b t p", t=4)[:, t, :]
+            exp_total = psum.tile([P, P], F32, tag="sums", bufs=3)
+            exps = []
+            for part in range(HALVES):
+                steps = slice(part * S_HALF, (part + 1) * S_HALF)
+                exps_h = work.tile([P, S_HALF, P], F32, tag="half_v", bufs=3)
+                nc.vector.tensor_tensor(
+                    out=exps_h[:], in0=enc_c[:, steps, :],
+                    in1=lin_c.unsqueeze(1).to_broadcast([P, S_HALF, P]), op=ALU.mult,
+                )
+                nc.vector.tensor_tensor(
+                    out=exps_h[:], in0=exps_h[:],
+                    in1=neg_peak_c.unsqueeze(1).to_broadcast([P, S_HALF, P]), op=ALU.add,
+                )
+                nc.scalar.activation(out=exps_h[:], in_=exps_h[:], func=ACT.Exp)
+                sum_over_s(exp_total, exps_h, part)
+                exps.append(exps_h)
+            inverse = work.tile([P, P], F32, tag="inverse")
+            nc.vector.reciprocal(out=inverse[:], in_=exp_total[:])
+            total = psum.tile([P, P], F32, tag="sums", bufs=3)
+            for part in range(HALVES):
+                steps = slice(part * S_HALF, (part + 1) * S_HALF)
+                terms = work.tile([P, S_HALF, P], F32, tag="half_v", bufs=3)
+                nc.vector.tensor_tensor(out=terms[:], in0=exps[part][:], in1=enc_c[:, steps, :], op=ALU.mult)
+                sum_over_s(total, terms, part)
+            nc.vector.tensor_tensor(out=mean, in0=total[:], in1=inverse[:], op=ALU.mult)
+
+        neg_peaks = [work.tile([P, K_PASS], F32, tag="neg_peak", name="neg_peak") for g in range(H_PASSES)]
+        for part in range(K_PASS // PEAK_FEATS):
+            negated_peaks(0, part, neg_peaks[0])
+        for r in range(ROUNDS):
+            g, u = divmod(r, 2)
+            if u == 0:
+                att_t = work.tile([P, 4, P], F32, tag="att_t", bufs=1)
+            gate_block(2 * r)
+            gate_block(2 * r + 1)
+
+            attention_by_vector(g, 2 * u, neg_peaks[g], att_t[:, 2 * u, :])
+
+            if g == 0:
+                if u == 0:
+                    enc_passes.append(load_enc_pass(1))
+                negated_peaks(1, u, neg_peaks[1])
+            inverse = attention_by_scalar(g, 2 * u + 1, neg_peaks[g], att_t[:, 2 * u + 1, :])
+
+            if u == 1:
+                att_grouped = work.tile([P, P, 4], BF16, tag="att_grouped", bufs=1, align_bytes=64)
+                nc.vector.tensor_copy(out=att_grouped[:], in_=att_t[:].rearrange("p t b -> p b t"))
+                nc.vector.quantize_mx(
+                    out=att_codes[:, g, :].bitcast(FP8X4),
+                    scales=att_planes[:, g, :],
+                    in_=att_grouped[:].rearrange("p b t -> p (b t)"),
+                )
+
+        warm = work.tile([P, 1], F32, tag="warm", bufs=1)
+        nc.scalar.activation(out=warm[:], in_=inverse[:, 0:1], func=ACT.Sigmoid)
+
+        for part in range(H_BLOCKS):
+            cols = slice(part * N_BLOCK, (part + 1) * N_BLOCK)
+            cell = work.tile([P, 4, N_BLOCK], F32, tag="half_v", bufs=3)
+            state = work.tile([P, 4, N_BLOCK], F32, tag="half_s", bufs=2)
+            for gate in range(4):
+                nb = gate * H_BLOCKS + part
+                acc = psum.tile([P, N_BLOCK], F32, tag="acc")
+                for g in range(H_PASSES):
+                    nc.tensor.matmul_mx(
+                        out=acc[:],
+                        lhsT=att_codes[:, g, :].bitcast(FP8X4),
+                        lhsT_scale=att_planes[:, g, :],
+                        rhs=wa_codes[:, nb, g, :].bitcast(FP8X4),
+                        rhs_scale=wa_plane(nb, g),
+                        start=(g == 0),
+                        stop=(g == H_PASSES - 1),
+                    )
+                nc.vector.tensor_tensor(
+                    out=cell[:, gate, :], in0=acc[:], in1=gates_xh[:, nb * N_BLOCK : (nb + 1) * N_BLOCK], op=ALU.add
+                )
+                nc.scalar.activation(
+                    out=cell[:, gate, :], in_=cell[:, gate, :], func=(ACT.Tanh if gate == 2 else ACT.Sigmoid)
+                )
+            gate_i, gate_f, gate_g, gate_o = [cell[:, gate, :] for gate in range(4)]
+            kept, c_new, tanh_c, h_new = [state[:, i, :] for i in range(4)]
+            nc.vector.tensor_tensor(out=kept, in0=gate_f, in1=c_sb[:, cols], op=ALU.mult)
+            nc.vector.tensor_tensor(out=c_new, in0=gate_i, in1=gate_g, op=ALU.mult)
+            nc.vector.tensor_tensor(out=c_new, in0=c_new, in1=kept, op=ALU.add)
+            nc.sync.dma_start(out=out_1[:, cols], in_=c_new)
+            nc.scalar.activation(out=tanh_c, in_=c_new, func=ACT.Tanh)
+            nc.vector.tensor_tensor(out=h_new, in0=gate_o, in1=tanh_c, op=ALU.mult)
+            nc.sync.dma_start(out=out_0[:, cols], in_=h_new)

@@ -32,9 +32,9 @@ HALVES = S // S_HALF
 FLOPS = 2 * P * (H * H + 4 * H * 3 * H)
 
 
-def load_weight_rows(nc, stage, rows):
+def load_weight_rows(nc, stage, rows, order="(t p) k -> p t k"):
     w_rows = stage.tile([P, ROW_TILES, H], BF16, tag="w_rows", bufs=3)
-    nc.sync.dma_start(out=w_rows[:], in_=rows.rearrange("(t p) k -> p t k", p=P))
+    nc.sync.dma_start(out=w_rows[:], in_=rows.rearrange(order, p=P))
     return w_rows[:].bitcast(F32)
 
 
@@ -125,7 +125,7 @@ def tile_decoderlstm_pa_kernel(
         x_sb = stage.tile([P, H], BF16, tag="w_rows", bufs=3)
         nc.sync.dma_start(out=x_sb[:], in_=x)
         attn_w_words = [
-            load_weight_rows(nc, stage, attn_W[nb * N_BLOCK : (nb + 1) * N_BLOCK, :]) for nb in range(H_BLOCKS)
+            load_weight_rows(nc, stage, attn_W[nb * N_BLOCK : (nb + 1) * N_BLOCK, :], "(p t) k -> p t k") for nb in range(H_BLOCKS)
         ]
         bias_rows = work.tile([P, 4 * H], BF16, tag="half_s", bufs=2)
         attn_b_rows = work.tile([P, H], BF16, tag="half_v", bufs=3)
@@ -154,7 +154,9 @@ def tile_decoderlstm_pa_kernel(
                 out=spread[:], lhsT=ones[:], rhs=attn_b_rows[:, cols],
                 start=True, stop=True,
             )
-            nc.scalar.copy(out=attn_lin[:, cols], in_=spread[:])
+            nc.scalar.copy(
+                out=attn_lin[:, cols].rearrange("b (t p) -> b t p", p=P), in_=spread[:].rearrange("b (p t) -> b t p", p=P)
+            )
             acc = psum.tile([P, N_BLOCK], F32, tag="acc")
             multiply_passes(nc, psum, stage, ident, acc, [(attn_w_words[nb], x_codes, x_planes)])
             nc.vector.tensor_tensor(out=attn_lin[:, cols], in0=acc[:], in1=attn_lin[:, cols], op=ALU.add)
@@ -193,10 +195,14 @@ def tile_decoderlstm_pa_kernel(
                     wa_codes[:, nb, g, :], wa_plane(nb, g),
                 )
 
+        def lin_chunks(g):
+            return attn_lin[:, g * K_PASS : (g + 1) * K_PASS].rearrange("b (t p) -> b t p", p=P)
+
         def negated_peaks(g, part, neg_peak):
             here = slice(part * PEAK_FEATS, (part + 1) * PEAK_FEATS)
             enc = enc_passes[g][:, :, here]
-            feats = slice(g * K_PASS + part * PEAK_FEATS, g * K_PASS + (part + 1) * PEAK_FEATS)
+            there = slice(part * PEAK_FEATS // 4, (part + 1) * PEAK_FEATS // 4)
+            lin = lin_chunks(g)[:, :, there]
             top = work.tile([P, QUARTER, PEAK_FEATS], BF16, tag="top", bufs=1)
             low = work.tile([P, QUARTER, PEAK_FEATS], BF16, tag="low", bufs=1)
             nc.vector.tensor_tensor(out=top[:], in0=enc[:, 0:QUARTER, :], in1=enc[:, QUARTER : 2 * QUARTER, :], op=ALU.max)
@@ -210,15 +216,14 @@ def tile_decoderlstm_pa_kernel(
                 nc.vector.tensor_tensor(out=top[:, 0:half, :], in0=top[:, 0:half, :], in1=top[:, half : 2 * half, :], op=ALU.max)
                 nc.vector.tensor_tensor(out=low[:, 0:half, :], in0=low[:, 0:half, :], in1=low[:, half : 2 * half, :], op=ALU.min)
                 half //= 2
-            neg_top = work.tile([P, PEAK_FEATS], F32, tag="neg_top", bufs=1)
-            neg_low = work.tile([P, PEAK_FEATS], F32, tag="neg_low", bufs=1)
-            nc.vector.scalar_tensor_tensor(
-                out=neg_top[:], in0=attn_lin[:, feats], scalar=-1.0, in1=top[:, 0, :], op0=ALU.mult, op1=ALU.mult
-            )
-            nc.vector.scalar_tensor_tensor(
-                out=neg_low[:], in0=attn_lin[:, feats], scalar=-1.0, in1=low[:, 0, :], op0=ALU.mult, op1=ALU.mult
-            )
-            nc.vector.tensor_tensor(out=neg_peak[:, here], in0=neg_top[:], in1=neg_low[:], op=ALU.min)
+            neg_top = work.tile([P, 4, PEAK_FEATS // 4], F32, tag="neg_top", bufs=1)
+            neg_low = work.tile([P, 4, PEAK_FEATS // 4], F32, tag="neg_low", bufs=1)
+            for neg, extreme in ((neg_top, top), (neg_low, low)):
+                nc.vector.scalar_tensor_tensor(
+                    out=neg[:], in0=lin, scalar=-1.0, in1=extreme[:, 0, :].rearrange("b (p t) -> b t p", t=4),
+                    op0=ALU.mult, op1=ALU.mult,
+                )
+            nc.vector.tensor_tensor(out=neg_peak[:, :, there], in0=neg_top[:], in1=neg_low[:], op=ALU.min)
 
         def chunk_of(g, t):
             return enc_passes[g][:].rearrange("b s (p t) -> b s t p", t=4)[:, :, t, :]
@@ -245,8 +250,8 @@ def tile_decoderlstm_pa_kernel(
                         out=exps_h[:, i, :],
                         in_=enc[:, :, j],
                         func=ACT.Exp,
-                        scale=attn_lin[:, g * K_PASS + j : g * K_PASS + j + 1],
-                        bias=neg_peak[:, j : j + 1],
+                        scale=lin_chunks(g)[:, t, p : p + 1],
+                        bias=neg_peak[:, t, p : p + 1],
                         accum_out=exp_sum[:, p : p + 1],
                     )
                 exps.append(exps_h)
@@ -272,8 +277,8 @@ def tile_decoderlstm_pa_kernel(
 
         def attention_by_vector(g, t, neg_peak, mean):
             enc_c = chunk_of(g, t)
-            lin_c = attn_lin[:, g * K_PASS : (g + 1) * K_PASS].rearrange("b (p t) -> b t p", t=4)[:, t, :]
-            neg_peak_c = neg_peak[:].rearrange("b (p t) -> b t p", t=4)[:, t, :]
+            lin_c = lin_chunks(g)[:, t, :]
+            neg_peak_c = neg_peak[:, t, :]
             exp_total = psum.tile([P, P], F32, tag="sums", bufs=3)
             exps = []
             for part in range(HALVES):
@@ -300,7 +305,7 @@ def tile_decoderlstm_pa_kernel(
                 sum_over_s(total, terms, part)
             nc.vector.tensor_tensor(out=mean, in0=total[:], in1=inverse[:], op=ALU.mult)
 
-        neg_peaks = [work.tile([P, K_PASS], F32, tag="neg_peak", name="neg_peak") for g in range(H_PASSES)]
+        neg_peaks = [work.tile([P, 4, P], F32, tag="neg_peak", name="neg_peak") for g in range(H_PASSES)]
         for part in range(K_PASS // PEAK_FEATS):
             negated_peaks(0, part, neg_peaks[0])
         for r in range(ROUNDS):

@@ -22,9 +22,9 @@ N_BLOCK = 512
 ROW_TILES = N_BLOCK // P
 H_BLOCKS = H // N_BLOCK
 GATE_BLOCKS = 4 * H_BLOCKS
-ROUNDS = 4
+CHUNKS = 8
+HALF_CHUNK = P // 2
 PEAK_FEATS = K_PASS // 2
-SCALAR_PART = P // 2
 QUARTER = S // 4
 S_HALF = S // 2
 HALVES = S // S_HALF
@@ -127,8 +127,8 @@ def tile_decoderlstm_pa_kernel(
         attn_w_words = [
             load_weight_rows(nc, stage, attn_W[nb * N_BLOCK : (nb + 1) * N_BLOCK, :], "(p t) k -> p t k") for nb in range(H_BLOCKS)
         ]
-        bias_rows = work.tile([P, 4 * H], BF16, tag="half_s", bufs=2)
-        attn_b_rows = work.tile([P, H], BF16, tag="half_v", bufs=3)
+        bias_rows = work.tile([P, 4 * H], BF16, tag="half_v", bufs=2)
+        attn_b_rows = work.tile([P, H], BF16, tag="half_v", bufs=2)
         nc.vector.memset(bias_rows[:].bitcast(I32), 0)
         nc.vector.memset(attn_b_rows[:].bitcast(I32), 0)
         nc.sync.dma_start(out=attn_b_rows[0:1, :], in_=attn_b.rearrange("(o n) -> o n", o=1))
@@ -236,94 +236,56 @@ def tile_decoderlstm_pa_kernel(
                     start=(s == 0), stop=(s == S - 1),
                 )
 
-        def attention_by_scalar(g, t, neg_peak, mean):
+        exps_ring = keep.tile([P, 3 * HALF_CHUNK, S], F32)
+
+        def attention_chunk(c, mean):
+            g, t = divmod(c, 4)
             enc = enc_passes[g]
             enc_c = chunk_of(g, t)
-            exp_sum = work.tile([P, P], F32, tag="exp_sum")
-            exps = []
-            for half in range(P // SCALAR_PART):
-                exps_h = work.tile([P, SCALAR_PART, S], F32, tag="half_s", bufs=2)
-                for i in range(SCALAR_PART):
-                    p = half * SCALAR_PART + i
-                    j = 4 * p + t
+            odd = c % 2
+            exps = exps_ring[:, odd * HALF_CHUNK : odd * HALF_CHUNK + P, :]
+            for half in ((1, 0) if odd else (0, 1)):
+                for p in range(half * HALF_CHUNK, (half + 1) * HALF_CHUNK):
                     nc.scalar.activation(
-                        out=exps_h[:, i, :],
-                        in_=enc[:, :, j],
+                        out=exps[:, p, :],
+                        in_=enc[:, :, 4 * p + t],
                         func=ACT.Exp,
                         scale=lin_chunks(g)[:, t, p : p + 1],
-                        bias=neg_peak[:, t, p : p + 1],
-                        accum_out=exp_sum[:, p : p + 1],
+                        bias=neg_peaks[g][:, t, p : p + 1],
                     )
-                exps.append(exps_h)
             exp_total = psum.tile([P, P], F32, tag="sums", bufs=3)
-            nc.tensor.transpose(exp_total[:], exp_sum[:], ident[:])
+            for part in range(HALVES):
+                sum_over_s(exp_total, exps[:, :, part * S_HALF : (part + 1) * S_HALF].rearrange("b p s -> b s p"), part)
             inverse = work.tile([P, P], F32, tag="inverse")
             nc.vector.reciprocal(out=inverse[:], in_=exp_total[:])
             total = psum.tile([P, P], F32, tag="sums", bufs=3)
             for part in range(HALVES):
                 steps = slice(part * S_HALF, (part + 1) * S_HALF)
-                terms = work.tile([P, S_HALF, P], F32, tag="half_v", bufs=3)
-                for half in range(P // SCALAR_PART):
-                    cols = slice(half * SCALAR_PART, (half + 1) * SCALAR_PART)
-                    nc.vector.tensor_tensor(
-                        out=terms[:, :, cols].rearrange("b (h l) p -> b h p l", l=2),
-                        in0=exps[half][:, :, steps].rearrange("b p (h l) -> b h p l", l=2),
-                        in1=enc_c[:, steps, cols].rearrange("b (h l) p -> b h p l", l=2),
-                        op=ALU.mult,
-                    )
+                terms = work.tile([P, S_HALF, P], F32, tag="half_v", bufs=2)
+                nc.vector.tensor_tensor(
+                    out=terms[:].rearrange("b (h l) p -> b h p l", l=2),
+                    in0=exps[:, :, steps].rearrange("b p (h l) -> b h p l", l=2),
+                    in1=enc_c[:, steps, :].rearrange("b (h l) p -> b h p l", l=2),
+                    op=ALU.mult,
+                )
                 sum_over_s(total, terms, part)
             nc.vector.tensor_tensor(out=mean, in0=total[:], in1=inverse[:], op=ALU.mult)
             return inverse
 
-        def attention_by_vector(g, t, neg_peak, mean):
-            enc_c = chunk_of(g, t)
-            lin_c = lin_chunks(g)[:, t, :]
-            neg_peak_c = neg_peak[:, t, :]
-            exp_total = psum.tile([P, P], F32, tag="sums", bufs=3)
-            exps = []
-            for part in range(HALVES):
-                steps = slice(part * S_HALF, (part + 1) * S_HALF)
-                exps_h = work.tile([P, S_HALF, P], F32, tag="half_v", bufs=3)
-                nc.vector.tensor_tensor(
-                    out=exps_h[:], in0=enc_c[:, steps, :],
-                    in1=lin_c.unsqueeze(1).to_broadcast([P, S_HALF, P]), op=ALU.mult,
-                )
-                nc.vector.tensor_tensor(
-                    out=exps_h[:], in0=exps_h[:],
-                    in1=neg_peak_c.unsqueeze(1).to_broadcast([P, S_HALF, P]), op=ALU.add,
-                )
-                nc.scalar.activation(out=exps_h[:], in_=exps_h[:], func=ACT.Exp)
-                sum_over_s(exp_total, exps_h, part)
-                exps.append(exps_h)
-            inverse = work.tile([P, P], F32, tag="inverse")
-            nc.vector.reciprocal(out=inverse[:], in_=exp_total[:])
-            total = psum.tile([P, P], F32, tag="sums", bufs=3)
-            for part in range(HALVES):
-                steps = slice(part * S_HALF, (part + 1) * S_HALF)
-                terms = work.tile([P, S_HALF, P], F32, tag="half_v", bufs=3)
-                nc.vector.tensor_tensor(out=terms[:], in0=exps[part][:], in1=enc_c[:, steps, :], op=ALU.mult)
-                sum_over_s(total, terms, part)
-            nc.vector.tensor_tensor(out=mean, in0=total[:], in1=inverse[:], op=ALU.mult)
-
         neg_peaks = [work.tile([P, 4, P], F32, tag="neg_peak", name="neg_peak") for g in range(H_PASSES)]
         for part in range(K_PASS // PEAK_FEATS):
             negated_peaks(0, part, neg_peaks[0])
-        for r in range(ROUNDS):
-            g, u = divmod(r, 2)
-            if u == 0:
+        for c in range(CHUNKS):
+            g, t = divmod(c, 4)
+            if t == 0:
                 att_t = work.tile([P, 4, P], F32, tag="att_t", bufs=1)
-            gate_block(2 * r)
-            gate_block(2 * r + 1)
-
-            attention_by_vector(g, 2 * u, neg_peaks[g], att_t[:, 2 * u, :])
-
-            if g == 0:
-                if u == 0:
-                    enc_passes.append(load_enc_pass(1))
-                negated_peaks(1, u, neg_peaks[1])
-            inverse = attention_by_scalar(g, 2 * u + 1, neg_peaks[g], att_t[:, 2 * u + 1, :])
-
-            if u == 1:
+            gate_block(c)
+            if c == 0:
+                enc_passes.append(load_enc_pass(1))
+            inverse = attention_chunk(c, att_t[:, t, :])
+            if c in (1, 2):
+                negated_peaks(1, c - 1, neg_peaks[1])
+            if t == 3:
                 att_grouped = work.tile([P, P, 4], BF16, tag="att_grouped", bufs=1, align_bytes=64)
                 nc.vector.tensor_copy(out=att_grouped[:], in_=att_t[:].rearrange("p t b -> p b t"))
                 nc.vector.quantize_mx(
@@ -337,8 +299,7 @@ def tile_decoderlstm_pa_kernel(
 
         for part in range(H_BLOCKS):
             cols = slice(part * N_BLOCK, (part + 1) * N_BLOCK)
-            cell = work.tile([P, 4, N_BLOCK], F32, tag="half_v", bufs=3)
-            state = work.tile([P, 4, N_BLOCK], F32, tag="half_s", bufs=2)
+            cell = work.tile([P, 8, N_BLOCK], F32, tag="enc")
             for gate in range(4):
                 nb = gate * H_BLOCKS + part
                 acc = psum.tile([P, N_BLOCK], F32, tag="acc")
@@ -359,7 +320,7 @@ def tile_decoderlstm_pa_kernel(
                     out=cell[:, gate, :], in_=cell[:, gate, :], func=(ACT.Tanh if gate == 2 else ACT.Sigmoid)
                 )
             gate_i, gate_f, gate_g, gate_o = [cell[:, gate, :] for gate in range(4)]
-            kept, c_new, tanh_c, h_new = [state[:, i, :] for i in range(4)]
+            kept, c_new, tanh_c, h_new = [cell[:, 4 + i, :] for i in range(4)]
             nc.vector.tensor_tensor(out=kept, in0=gate_f, in1=c_sb[:, cols], op=ALU.mult)
             nc.vector.tensor_tensor(out=c_new, in0=gate_i, in1=gate_g, op=ALU.mult)
             nc.vector.tensor_tensor(out=c_new, in0=c_new, in1=kept, op=ALU.add)

@@ -5,7 +5,6 @@ from concourse.masks import make_identity
 
 F32 = mybir.dt.float32
 BF16 = mybir.dt.bfloat16
-I32 = mybir.dt.int32
 U32 = mybir.dt.uint32
 U8 = mybir.dt.uint8
 FP8X4 = mybir.dt.float8_e4m3fn_x4
@@ -24,6 +23,8 @@ H_BLOCKS = H // N_BLOCK
 GATE_BLOCKS = 4 * H_BLOCKS
 CHUNKS = 8
 HALF_CHUNK = P // 2
+ENC_PITCH = K_PASS + 8
+EXPS_PITCH = S + 4
 PEAK_FEATS = K_PASS // 2
 QUARTER = S // 4
 S_HALF = S // 2
@@ -108,65 +109,63 @@ def tile_decoderlstm_pa_kernel(
         work = stack.enter_context(tc.tile_pool(name="work", bufs=2))
         psum = stack.enter_context(tc.psum_pool(name="psum", bufs=2))
 
-        def load_enc_pass(g):
-            enc = work.tile([P, S, K_PASS], BF16, tag="enc")
+        def load_enc_steps(g, quarters):
+            if len(enc_passes) == g:
+                enc_passes.append(work.tile([P, S, ENC_PITCH], BF16, tag="enc", name="enc"))
             feats = slice(g * K_PASS, (g + 1) * K_PASS)
-            for i in range(S // QUARTER):
+            for i in quarters:
                 steps = slice(i * QUARTER, (i + 1) * QUARTER)
-                nc.sync.dma_start(out=enc[:, steps, :], in_=enc_seq[steps, :, feats].rearrange("s b j -> b s j"))
-            return enc
+                nc.sync.dma_start(out=enc_passes[g][:, steps, 0:K_PASS], in_=enc_seq[steps, :, feats].rearrange("s b j -> b s j"))
 
         ident = const.tile([P, P], F32)
         make_identity(nc, ident[:])
-        ones = const.tile([P, P], BF16)
-        nc.vector.memset(ones[:], 1.0)
+        warm_exp = const.tile([P, 1], F32)
+        nc.scalar.activation(out=warm_exp[:], in_=ident[:, 0:1], func=ACT.Exp)
 
-        enc_passes = [load_enc_pass(0)]
-        x_sb = stage.tile([P, H], BF16, tag="w_rows", bufs=3)
+        x_sb = stage.tile([P, H], BF16, tag="act_rows", bufs=3)
         nc.sync.dma_start(out=x_sb[:], in_=x)
-        attn_w_words = [
-            load_weight_rows(nc, stage, attn_W[nb * N_BLOCK : (nb + 1) * N_BLOCK, :], "(p t) k -> p t k") for nb in range(H_BLOCKS)
-        ]
-        bias_rows = work.tile([P, 4 * H], BF16, tag="half_v", bufs=2)
-        attn_b_rows = work.tile([P, H], BF16, tag="half_v", bufs=2)
-        nc.vector.memset(bias_rows[:].bitcast(I32), 0)
-        nc.vector.memset(attn_b_rows[:].bitcast(I32), 0)
-        nc.sync.dma_start(out=attn_b_rows[0:1, :], in_=attn_b.rearrange("(o n) -> o n", o=1))
-        nc.sync.dma_start(out=bias_rows[0:1, 0 : 4 * H], in_=b_ih0.rearrange("(o n) -> o n", o=1))
-        nc.sync.dma_start(out=bias_rows[1:2, 0 : 4 * H], in_=b_hh0.rearrange("(o n) -> o n", o=1))
-        h_sb = stage.tile([P, H], BF16, tag="act_rows", bufs=1)
+        enc_passes = []
+        load_enc_steps(0, range(2))
+        attn_w_words = [load_weight_rows(nc, stage, attn_W[0:N_BLOCK, :], "(p t) k -> p t k")]
+        attn_b_all = stage.tile([P, H], BF16, tag="act_rows", bufs=3)
+        nc.sync.dma_start(out=attn_b_all[:], in_=attn_b.partition_broadcast(P))
+        load_enc_steps(0, range(2, 4))
+        attn_w_words.append(load_weight_rows(nc, stage, attn_W[N_BLOCK:H, :], "(p t) k -> p t k"))
+        h_sb = stage.tile([P, H], BF16, tag="act_rows", bufs=3)
         nc.sync.dma_start(out=h_sb[:], in_=h_prev)
-        c_sb = keep.tile([P, H], BF16)
-        nc.sync.dma_start(out=c_sb[:], in_=c_prev)
+
+        biases = [work.tile([P, 4 * H // P], BF16, tag="bias", name="bias") for i in range(2)]
+        for bias, b_hbm in zip(biases, (b_ih0, b_hh0)):
+            nc.gpsimd.dma_start(out=bias[:], in_=b_hbm.rearrange("(p n) -> p n", p=P))
+        bias_sum = work.tile([P, 4 * H // P], F32, tag="bias_sum", bufs=1)
+        nc.gpsimd.tensor_tensor(out=bias_sum[:], in0=biases[0][:], in1=biases[1][:], op=ALU.add)
+        parked = out_0[0:4, :].rearrange("r n -> (r n)")
+        nc.gpsimd.dma_start(out=parked.rearrange("(p n) -> p n", p=P), in_=bias_sum[:])
+        gates_xh = keep.tile([P, 4 * H], F32)
 
         x_codes = keep.tile([P, H_PASSES, P], U32, align_bytes=64)
         x_planes = keep.tile([P, H_PASSES, P], U8, align_bytes=64)
         quantise_activations(nc, psum, stage, ident, x_sb, x_codes, x_planes)
         h_codes = keep.tile([P, H_PASSES, P], U32, align_bytes=64)
         h_planes = keep.tile([P, H_PASSES, P], U8, align_bytes=64)
-        quantise_activations(nc, psum, stage, ident, h_sb, h_codes, h_planes)
 
         attn_lin = keep.tile([P, H], F32)
-        for nb in range(H_BLOCKS):
+
+        def attn_lin_block(nb):
             cols = slice(nb * N_BLOCK, (nb + 1) * N_BLOCK)
-            spread = psum.tile([P, N_BLOCK], F32, tag="acc")
-            nc.tensor.matmul(
-                out=spread[:], lhsT=ones[:], rhs=attn_b_rows[:, cols],
-                start=True, stop=True,
-            )
-            nc.scalar.copy(
-                out=attn_lin[:, cols].rearrange("b (t p) -> b t p", p=P), in_=spread[:].rearrange("b (p t) -> b t p", p=P)
-            )
             acc = psum.tile([P, N_BLOCK], F32, tag="acc")
             multiply_passes(nc, psum, stage, ident, acc, [(attn_w_words[nb], x_codes, x_planes)])
-            nc.vector.tensor_tensor(out=attn_lin[:, cols], in0=acc[:], in1=attn_lin[:, cols], op=ALU.add)
+            nc.vector.tensor_tensor(
+                out=attn_lin[:, cols].rearrange("b (t p) -> b t p", p=P),
+                in0=acc[:].rearrange("b (t p) -> b t p", p=P),
+                in1=attn_b_all[:, cols].rearrange("b (p t) -> b t p", p=P),
+                op=ALU.add,
+            )
 
-        gates_xh = keep.tile([P, 4 * H], F32)
-        for nb in range(GATE_BLOCKS):
-            cols = slice(nb * N_BLOCK, (nb + 1) * N_BLOCK)
-            spread = psum.tile([P, N_BLOCK], F32, tag="acc")
-            nc.tensor.matmul(out=spread[:], lhsT=ones[:], rhs=bias_rows[:, cols], start=True, stop=True)
-            nc.scalar.copy(out=gates_xh[:, cols], in_=spread[:])
+        attn_lin_block(0)
+        attn_lin_block(1)
+        quantise_activations(nc, psum, stage, ident, h_sb, h_codes, h_planes)
+        c_sb = stage.tile([P, H], BF16, tag="act_rows", bufs=3)
 
         wa_codes = keep.tile([P, GATE_BLOCKS, H_PASSES, N_BLOCK], U32, align_bytes=64)
         wa_planes = keep.tile([P, GATE_BLOCKS // 2, N_BLOCK], U8, align_bytes=64)
@@ -178,11 +177,12 @@ def tile_decoderlstm_pa_kernel(
         att_codes = keep.tile([P, H_PASSES, P], U32, align_bytes=64)
         att_planes = keep.tile([P, H_PASSES, P], U8, align_bytes=64)
 
-        def gate_block(nb):
+        def load_gate_block(nb):
             rows = slice(nb * N_BLOCK, (nb + 1) * N_BLOCK)
-            wx_words = load_weight_rows(nc, stage, W_ih0[rows, 0:H])
-            wh_words = load_weight_rows(nc, stage, W_hh0[rows, :])
-            wa_words = load_weight_rows(nc, stage, W_ih0[rows, H : 2 * H])
+            return [load_weight_rows(nc, stage, w) for w in (W_ih0[rows, 0:H], W_hh0[rows, :], W_ih0[rows, H : 2 * H])]
+
+        def gate_block(nb, wx_words, wh_words, wa_words):
+            rows = slice(nb * N_BLOCK, (nb + 1) * N_BLOCK)
             acc = psum.tile([P, N_BLOCK], F32, tag="acc")
             multiply_passes(
                 nc, psum, stage, ident, acc, [(wx_words, x_codes, x_planes), (wh_words, h_codes, h_planes)]
@@ -226,7 +226,7 @@ def tile_decoderlstm_pa_kernel(
             nc.vector.tensor_tensor(out=neg_peak[:, :, there], in0=neg_top[:], in1=neg_low[:], op=ALU.min)
 
         def chunk_of(g, t):
-            return enc_passes[g][:].rearrange("b s (p t) -> b s t p", t=4)[:, :, t, :]
+            return enc_passes[g][:, :, 0:K_PASS].rearrange("b s (p t) -> b s t p", t=4)[:, :, t, :]
 
         def sum_over_s(total, tiles, part):
             for i in range(S_HALF):
@@ -236,14 +236,14 @@ def tile_decoderlstm_pa_kernel(
                     start=(s == 0), stop=(s == S - 1),
                 )
 
-        exps_ring = keep.tile([P, 3 * HALF_CHUNK, S], F32)
+        exps_ring = keep.tile([P, 3 * HALF_CHUNK, EXPS_PITCH], F32)
 
         def attention_chunk(c, mean):
             g, t = divmod(c, 4)
             enc = enc_passes[g]
             enc_c = chunk_of(g, t)
             odd = c % 2
-            exps = exps_ring[:, odd * HALF_CHUNK : odd * HALF_CHUNK + P, :]
+            exps = exps_ring[:, odd * HALF_CHUNK : odd * HALF_CHUNK + P, 0:S]
             for half in ((1, 0) if odd else (0, 1)):
                 for p in range(half * HALF_CHUNK, (half + 1) * HALF_CHUNK):
                     nc.scalar.activation(
@@ -279,9 +279,13 @@ def tile_decoderlstm_pa_kernel(
             g, t = divmod(c, 4)
             if t == 0:
                 att_t = work.tile([P, 4, P], F32, tag="att_t", bufs=1)
-            gate_block(c)
+            block_words = load_gate_block(c)
             if c == 0:
-                enc_passes.append(load_enc_pass(1))
+                nc.sync.dma_start(out=gates_xh[:], in_=parked.partition_broadcast(P))
+            gate_block(c, *block_words)
+            if c == 0:
+                load_enc_steps(1, range(4))
+                nc.sync.dma_start(out=c_sb[:], in_=c_prev)
             inverse = attention_chunk(c, att_t[:, t, :])
             if c in (1, 2):
                 negated_peaks(1, c - 1, neg_peaks[1])

@@ -22,9 +22,8 @@ ROW_TILES = N_BLOCK // P
 H_BLOCKS = H // N_BLOCK
 GATE_BLOCKS = 4 * H_BLOCKS
 CHUNKS = 8
-HALF_CHUNK = P // 2
-ENC_PITCH = K_PASS + 8
-EXPS_PITCH = S + 4
+SCALAR_PART = P // 2
+VECTOR_CHUNKS = (2, 4, 6)
 PEAK_FEATS = K_PASS // 2
 QUARTER = S // 4
 S_HALF = S // 2
@@ -111,11 +110,11 @@ def tile_decoderlstm_pa_kernel(
 
         def load_enc_steps(g, quarters):
             if len(enc_passes) == g:
-                enc_passes.append(work.tile([P, S, ENC_PITCH], BF16, tag="enc", name="enc"))
+                enc_passes.append(work.tile([P, S, K_PASS], BF16, tag="enc", name="enc"))
             feats = slice(g * K_PASS, (g + 1) * K_PASS)
             for i in quarters:
                 steps = slice(i * QUARTER, (i + 1) * QUARTER)
-                nc.sync.dma_start(out=enc_passes[g][:, steps, 0:K_PASS], in_=enc_seq[steps, :, feats].rearrange("s b j -> b s j"))
+                nc.sync.dma_start(out=enc_passes[g][:, steps, :], in_=enc_seq[steps, :, feats].rearrange("s b j -> b s j"))
 
         ident = const.tile([P, P], F32)
         make_identity(nc, ident[:])
@@ -226,7 +225,7 @@ def tile_decoderlstm_pa_kernel(
             nc.vector.tensor_tensor(out=neg_peak[:, :, there], in0=neg_top[:], in1=neg_low[:], op=ALU.min)
 
         def chunk_of(g, t):
-            return enc_passes[g][:, :, 0:K_PASS].rearrange("b s (p t) -> b s t p", t=4)[:, :, t, :]
+            return enc_passes[g][:].rearrange("b s (p t) -> b s t p", t=4)[:, :, t, :]
 
         def sum_over_s(total, tiles, part):
             for i in range(S_HALF):
@@ -236,38 +235,72 @@ def tile_decoderlstm_pa_kernel(
                     start=(s == 0), stop=(s == S - 1),
                 )
 
-        exps_ring = keep.tile([P, 3 * HALF_CHUNK, EXPS_PITCH], F32)
-
-        def attention_chunk(c, mean):
-            g, t = divmod(c, 4)
+        def attention_by_scalar(g, t, neg_peak, mean):
             enc = enc_passes[g]
             enc_c = chunk_of(g, t)
-            odd = c % 2
-            exps = exps_ring[:, odd * HALF_CHUNK : odd * HALF_CHUNK + P, 0:S]
-            for half in ((1, 0) if odd else (0, 1)):
-                for p in range(half * HALF_CHUNK, (half + 1) * HALF_CHUNK):
+            exp_sum = work.tile([P, P], F32, tag="exp_sum")
+            exps = []
+            for half in range(P // SCALAR_PART):
+                exps_h = work.tile([P, SCALAR_PART, S], F32, tag="half_s", bufs=2)
+                for i in range(SCALAR_PART):
+                    p = half * SCALAR_PART + i
+                    j = 4 * p + t
                     nc.scalar.activation(
-                        out=exps[:, p, :],
-                        in_=enc[:, :, 4 * p + t],
+                        out=exps_h[:, i, :],
+                        in_=enc[:, :, j],
                         func=ACT.Exp,
                         scale=lin_chunks(g)[:, t, p : p + 1],
-                        bias=neg_peaks[g][:, t, p : p + 1],
+                        bias=neg_peak[:, t, p : p + 1],
+                        accum_out=exp_sum[:, p : p + 1],
                     )
+                exps.append(exps_h)
             exp_total = psum.tile([P, P], F32, tag="sums", bufs=3)
-            for part in range(HALVES):
-                sum_over_s(exp_total, exps[:, :, part * S_HALF : (part + 1) * S_HALF].rearrange("b p s -> b s p"), part)
+            nc.tensor.transpose(exp_total[:], exp_sum[:], ident[:])
             inverse = work.tile([P, P], F32, tag="inverse")
             nc.vector.reciprocal(out=inverse[:], in_=exp_total[:])
             total = psum.tile([P, P], F32, tag="sums", bufs=3)
             for part in range(HALVES):
                 steps = slice(part * S_HALF, (part + 1) * S_HALF)
-                terms = work.tile([P, S_HALF, P], F32, tag="half_v", bufs=2)
+                terms = work.tile([P, S_HALF, P], F32, tag="half_v", bufs=3)
+                for half in range(P // SCALAR_PART):
+                    cols = slice(half * SCALAR_PART, (half + 1) * SCALAR_PART)
+                    nc.vector.tensor_tensor(
+                        out=terms[:, :, cols].rearrange("b (h l) p -> b h p l", l=2),
+                        in0=exps[half][:, :, steps].rearrange("b p (h l) -> b h p l", l=2),
+                        in1=enc_c[:, steps, cols].rearrange("b (h l) p -> b h p l", l=2),
+                        op=ALU.mult,
+                    )
+                sum_over_s(total, terms, part)
+            nc.vector.tensor_tensor(out=mean, in0=total[:], in1=inverse[:], op=ALU.mult)
+            return inverse
+
+        def attention_by_vector(g, t, neg_peak, mean):
+            enc_c = chunk_of(g, t)
+            lin_c = lin_chunks(g)[:, t, :]
+            neg_peak_c = neg_peak[:, t, :]
+            exp_total = psum.tile([P, P], F32, tag="sums", bufs=3)
+            exps = []
+            for part in range(HALVES):
+                steps = slice(part * S_HALF, (part + 1) * S_HALF)
+                exps_h = work.tile([P, S_HALF, P], F32, tag="half_v", bufs=3)
                 nc.vector.tensor_tensor(
-                    out=terms[:].rearrange("b (h l) p -> b h p l", l=2),
-                    in0=exps[:, :, steps].rearrange("b p (h l) -> b h p l", l=2),
-                    in1=enc_c[:, steps, :].rearrange("b (h l) p -> b h p l", l=2),
-                    op=ALU.mult,
+                    out=exps_h[:], in0=enc_c[:, steps, :],
+                    in1=lin_c.unsqueeze(1).to_broadcast([P, S_HALF, P]), op=ALU.mult,
                 )
+                nc.vector.tensor_tensor(
+                    out=exps_h[:], in0=exps_h[:],
+                    in1=neg_peak_c.unsqueeze(1).to_broadcast([P, S_HALF, P]), op=ALU.add,
+                )
+                nc.scalar.activation(out=exps_h[:], in_=exps_h[:], func=ACT.Exp)
+                sum_over_s(exp_total, exps_h, part)
+                exps.append(exps_h)
+            inverse = work.tile([P, P], F32, tag="inverse")
+            nc.vector.reciprocal(out=inverse[:], in_=exp_total[:])
+            total = psum.tile([P, P], F32, tag="sums", bufs=3)
+            for part in range(HALVES):
+                steps = slice(part * S_HALF, (part + 1) * S_HALF)
+                terms = work.tile([P, S_HALF, P], F32, tag="half_v", bufs=3)
+                nc.vector.tensor_tensor(out=terms[:], in0=exps[part][:], in1=enc_c[:, steps, :], op=ALU.mult)
                 sum_over_s(total, terms, part)
             nc.vector.tensor_tensor(out=mean, in0=total[:], in1=inverse[:], op=ALU.mult)
             return inverse
@@ -286,7 +319,8 @@ def tile_decoderlstm_pa_kernel(
             if c == 0:
                 load_enc_steps(1, range(4))
                 nc.sync.dma_start(out=c_sb[:], in_=c_prev)
-            inverse = attention_chunk(c, att_t[:, t, :])
+            attention = attention_by_vector if c in VECTOR_CHUNKS else attention_by_scalar
+            inverse = attention(g, t, neg_peaks[g], att_t[:, t, :])
             if c in (1, 2):
                 negated_peaks(1, c - 1, neg_peaks[1])
             if t == 3:

@@ -21,11 +21,32 @@ N_BLOCK = 512
 ROW_TILES = N_BLOCK // P
 H_BLOCKS = H // N_BLOCK
 GATE_BLOCKS = 4 * H_BLOCKS
+LATE_BLOCK = 7
+EARLY_BLOCKS = 4
+ATTN = -1
+ENC_LOADS = {0: range(0, 1), 1: range(1, 4)}
+ACC_BANKS = 1
+TURN_BANKS = 3
+SUM_BANKS = 4
 CHUNKS = 8
 SCALAR_PART = P // 2
 VECTOR_CHUNKS = (2, 4, 6)
-PEAK_FEATS = K_PASS // 2
+SCALAR_CHUNKS = (0, 1, 3, 5, 7)
+ACTS_A_STEP = 8
+SCALAR_START = 2
+FOLDS_IN_TURN = 5
+PEAKS_END = 6
+SCALAR_END = 88
+VECTOR_END = 76
+CELL_START = 92
+ACT_LAG = 1
+QUANTISE_LAG = 2
+MULTIPLY_LAG = 4
+SUM_LAG = 3
+EXP_LAG = 3
 QUARTER = S // 4
+PEAK_PART = P // 2
+FOLD = 4
 S_HALF = S // 2
 HALVES = S // S_HALF
 
@@ -33,68 +54,69 @@ FLOPS = 2 * P * (H * H + 4 * H * 3 * H)
 
 
 def load_weight_rows(nc, stage, rows, order="(t p) k -> p t k"):
-    w_rows = stage.tile([P, ROW_TILES, H], BF16, tag="w_rows", bufs=3)
+    w_rows = stage.tile([P, ROW_TILES, H], BF16, tag="w_rows", bufs=4)
     nc.sync.dma_start(out=w_rows[:], in_=rows.rearrange(order, p=P))
     return w_rows[:].bitcast(F32)
 
 
-def quantise_weight_pass(nc, psum, stage, ident, words, codes, plane):
+def new_grouped(stage):
     grouped = stage.tile([P, 4 * N_BLOCK], BF16, tag="grouped", bufs=3, align_bytes=64)
-    grouped_words = grouped[:].bitcast(F32).rearrange("p (r u) -> p r u", u=2)
-    for pair in range(ROW_TILES // 2):
-        bank = psum.tile([P, 2, 2 * P], F32, tag="wt", bufs=3)
-        for i in range(2):
-            for u in range(2):
-                nc.tensor.transpose(
-                    bank[:, u, i * P : (i + 1) * P],
-                    words[:, 2 * pair + i, u : PASS_WORDS : 2],
-                    ident[:],
-                )
-        nc.scalar.copy(
-            out=grouped_words[:, pair * 2 * P : (pair + 1) * 2 * P, :],
-            in_=bank[:].rearrange("p u r -> p r u"),
-        )
-    nc.vector.quantize_mx(out=codes.bitcast(FP8X4), scales=plane, in_=grouped[:])
+    return grouped
 
 
-def quantise_activations(nc, psum, stage, ident, rows, codes, planes):
-    words = rows[:].bitcast(F32)
-    bank = psum.tile([P, 2 * H_PASSES, P], F32, tag="wt", bufs=3)
-    for q in range(2 * H_PASSES):
-        nc.tensor.transpose(bank[:, q, :], words[:, (q // 2) * PASS_WORDS + q % 2 : (q // 2 + 1) * PASS_WORDS : 2], ident[:])
-    grouped = stage.tile([P, 4 * H_PASSES * P], BF16, tag="act_grouped", bufs=1, align_bytes=64)
-    nc.scalar.copy(
-        out=grouped[:].bitcast(F32).rearrange("p (g b u) -> p g b u", g=H_PASSES, u=2),
-        in_=bank[:].rearrange("p (g u) b -> p g b u", u=2),
-    )
-    nc.vector.quantize_mx(
-        out=codes[:].rearrange("p g b -> p (g b)").bitcast(FP8X4),
-        scales=planes[:].rearrange("p g b -> p (g b)"),
-        in_=grouped[:],
-    )
+def new_weight_operand(stage):
+    codes = stage.tile([P, N_BLOCK], U32, tag="w_codes", bufs=4, align_bytes=64)
+    plane = stage.tile([P, N_BLOCK], U8, tag="w_plane", bufs=4, align_bytes=64)
+    return codes[:], plane[:]
 
 
-def multiply_passes(nc, psum, stage, ident, acc, operands):
-    passes = []
-    for w_words, act_codes, act_planes in operands:
-        for g in range(H_PASSES):
-            w_codes = stage.tile([P, N_BLOCK], U32, tag="w_codes", bufs=4, align_bytes=64)
-            w_plane = stage.tile([P, N_BLOCK], U8, tag="w_plane", bufs=4, align_bytes=64)
-            quantise_weight_pass(
-                nc, psum, stage, ident,
-                w_words[:, :, g * PASS_WORDS : (g + 1) * PASS_WORDS], w_codes[:], w_plane[:],
+def transpose_half(nc, psum, ident, words, pair, grouped):
+    bank = psum.tile([P, 2, 2 * P], F32, tag="wt", bufs=TURN_BANKS)
+    for i in range(2):
+        for u in range(2):
+            nc.tensor.transpose(
+                bank[:, u, i * P : (i + 1) * P], words[:, 2 * pair + i, u : PASS_WORDS : 2], ident[:]
             )
-            passes.append((act_codes[:, g, :], act_planes[:, g, :], w_codes, w_plane))
+    grouped_words = grouped[:].bitcast(F32).rearrange("p (r u) -> p r u", u=2)
+    nc.scalar.copy(
+        out=grouped_words[:, pair * 2 * P : (pair + 1) * 2 * P, :], in_=bank[:].rearrange("p u r -> p r u")
+    )
+
+
+def multiply(nc, acc, passes, start=True, stop=True):
     for i, (a_codes, a_plane, w_codes, w_plane) in enumerate(passes):
         nc.tensor.matmul_mx(
             out=acc[:],
             lhsT=a_codes.bitcast(FP8X4),
             lhsT_scale=a_plane,
-            rhs=w_codes[:].bitcast(FP8X4),
-            rhs_scale=w_plane[:],
-            start=(i == 0),
-            stop=(i == len(passes) - 1),
+            rhs=w_codes.bitcast(FP8X4),
+            rhs_scale=w_plane,
+            start=(start and i == 0),
+            stop=(stop and i == len(passes) - 1),
         )
+
+
+def turn_activations(nc, psum, stage, ident, rows):
+    words = rows[:].bitcast(F32)
+    bank = psum.tile([P, 2 * H_PASSES, P], F32, tag="wt", bufs=TURN_BANKS)
+    for q in range(2 * H_PASSES):
+        nc.tensor.transpose(
+            bank[:, q, :], words[:, (q // 2) * PASS_WORDS + q % 2 : (q // 2 + 1) * PASS_WORDS : 2], ident[:]
+        )
+    grouped = stage.tile([P, 4 * H_PASSES * P], BF16, tag="grouped", bufs=3, align_bytes=64)
+    nc.scalar.copy(
+        out=grouped[:].bitcast(F32).rearrange("p (g b u) -> p g b u", g=H_PASSES, u=2),
+        in_=bank[:].rearrange("p (g u) b -> p g b u", u=2),
+    )
+    return grouped
+
+
+def quantise_activations(nc, grouped, codes, planes):
+    nc.vector.quantize_mx(
+        out=codes[:].rearrange("p g b -> p (g b)").bitcast(FP8X4),
+        scales=planes[:].rearrange("p g b -> p (g b)"),
+        in_=grouped[:],
+    )
 
 
 def tile_decoderlstm_pa_kernel(
@@ -110,28 +132,27 @@ def tile_decoderlstm_pa_kernel(
 
         def load_enc_steps(g, quarters):
             if len(enc_passes) == g:
-                enc_passes.append(work.tile([P, S, K_PASS], BF16, tag="enc", name="enc"))
+                enc_passes.append(work.tile([P, S, K_PASS], BF16, tag="enc", name="enc", align_bytes=64))
             feats = slice(g * K_PASS, (g + 1) * K_PASS)
             for i in quarters:
                 steps = slice(i * QUARTER, (i + 1) * QUARTER)
                 nc.sync.dma_start(out=enc_passes[g][:, steps, :], in_=enc_seq[steps, :, feats].rearrange("s b j -> b s j"))
+
+        def load_attn_rows(nb):
+            return load_weight_rows(nc, stage, attn_W[nb * N_BLOCK : (nb + 1) * N_BLOCK, :], "(p t) k -> p t k")
 
         ident = const.tile([P, P], F32)
         make_identity(nc, ident[:])
         warm_exp = const.tile([P, 1], F32)
         nc.scalar.activation(out=warm_exp[:], in_=ident[:, 0:1], func=ACT.Exp)
 
-        x_sb = stage.tile([P, H], BF16, tag="act_rows", bufs=3)
-        nc.sync.dma_start(out=x_sb[:], in_=x)
         enc_passes = []
-        load_enc_steps(0, range(2))
-        attn_w_words = [load_weight_rows(nc, stage, attn_W[0:N_BLOCK, :], "(p t) k -> p t k")]
-        attn_b_all = stage.tile([P, H], BF16, tag="act_rows", bufs=3)
+        x_sb = stage.tile([P, H], BF16, tag="act_rows", bufs=2)
+        nc.sync.dma_start(out=x_sb[:], in_=x)
+        load_enc_steps(0, range(3))
+        attn_words = load_attn_rows(0)
+        attn_b_all = stage.tile([P, H], BF16, tag="act_rows", bufs=2)
         nc.sync.dma_start(out=attn_b_all[:], in_=attn_b.partition_broadcast(P))
-        load_enc_steps(0, range(2, 4))
-        attn_w_words.append(load_weight_rows(nc, stage, attn_W[N_BLOCK:H, :], "(p t) k -> p t k"))
-        h_sb = stage.tile([P, H], BF16, tag="act_rows", bufs=3)
-        nc.sync.dma_start(out=h_sb[:], in_=h_prev)
 
         biases = [work.tile([P, 4 * H // P], BF16, tag="bias", name="bias") for i in range(2)]
         for bias, b_hbm in zip(biases, (b_ih0, b_hh0)):
@@ -144,16 +165,13 @@ def tile_decoderlstm_pa_kernel(
 
         x_codes = keep.tile([P, H_PASSES, P], U32, align_bytes=64)
         x_planes = keep.tile([P, H_PASSES, P], U8, align_bytes=64)
-        quantise_activations(nc, psum, stage, ident, x_sb, x_codes, x_planes)
         h_codes = keep.tile([P, H_PASSES, P], U32, align_bytes=64)
         h_planes = keep.tile([P, H_PASSES, P], U8, align_bytes=64)
 
         attn_lin = keep.tile([P, H], F32)
 
-        def attn_lin_block(nb):
+        def add_attn_bias(nb, acc):
             cols = slice(nb * N_BLOCK, (nb + 1) * N_BLOCK)
-            acc = psum.tile([P, N_BLOCK], F32, tag="acc")
-            multiply_passes(nc, psum, stage, ident, acc, [(attn_w_words[nb], x_codes, x_planes)])
             nc.vector.tensor_tensor(
                 out=attn_lin[:, cols].rearrange("b (t p) -> b t p", p=P),
                 in0=acc[:].rearrange("b (t p) -> b t p", p=P),
@@ -161,13 +179,17 @@ def tile_decoderlstm_pa_kernel(
                 op=ALU.add,
             )
 
-        attn_lin_block(0)
-        attn_lin_block(1)
-        quantise_activations(nc, psum, stage, ident, h_sb, h_codes, h_planes)
-        c_sb = stage.tile([P, H], BF16, tag="act_rows", bufs=3)
+        def load_c():
+            c_sb = stage.tile([P, H], BF16, tag="act_rows", bufs=2)
+            nc.sync.dma_start(out=c_sb[:], in_=c_prev)
+            now["c"] = c_sb
 
-        wa_codes = keep.tile([P, GATE_BLOCKS, H_PASSES, N_BLOCK], U32, align_bytes=64)
+        wa_codes = [keep.tile([P, EARLY_BLOCKS, H_PASSES, N_BLOCK], U32, align_bytes=64, name="wa_codes")]
         wa_planes = keep.tile([P, GATE_BLOCKS // 2, N_BLOCK], U8, align_bytes=64)
+
+        def wa_code(nb, g):
+            late, at = divmod(nb, EARLY_BLOCKS)
+            return wa_codes[late][:, at, g, :]
 
         def wa_plane(nb, g):
             row = 4 * (2 * (nb % 2) + g)
@@ -180,49 +202,91 @@ def tile_decoderlstm_pa_kernel(
             rows = slice(nb * N_BLOCK, (nb + 1) * N_BLOCK)
             return [load_weight_rows(nc, stage, w) for w in (W_ih0[rows, 0:H], W_hh0[rows, :], W_ih0[rows, H : 2 * H])]
 
-        def gate_block(nb, wx_words, wh_words, wa_words):
-            rows = slice(nb * N_BLOCK, (nb + 1) * N_BLOCK)
-            acc = psum.tile([P, N_BLOCK], F32, tag="acc")
-            multiply_passes(
-                nc, psum, stage, ident, acc, [(wx_words, x_codes, x_planes), (wh_words, h_codes, h_planes)]
+        now = {}
+        waiting = []
+
+        def weight_step(nb, kind, g, pair):
+            if (kind, g, pair) == (0, 0, 0):
+                now["words"] = [load_attn_rows(1)] if nb == ATTN else load_gate_block(nb)
+                if nb == 0:
+                    nc.sync.dma_start(out=gates_xh[:], in_=parked.partition_broadcast(P))
+                if nb in ENC_LOADS:
+                    load_enc_steps(1, ENC_LOADS[nb])
+            if pair == 0:
+                now["grouped"] = new_grouped(stage)
+            transpose_half(
+                nc, psum, ident, now["words"][kind][:, :, g * PASS_WORDS : (g + 1) * PASS_WORDS], pair, now["grouped"]
             )
-            nc.vector.tensor_tensor(out=gates_xh[:, rows], in0=acc[:], in1=gates_xh[:, rows], op=ALU.add)
-            for g in range(H_PASSES):
-                quantise_weight_pass(
-                    nc, psum, stage, ident,
-                    wa_words[:, :, g * PASS_WORDS : (g + 1) * PASS_WORDS],
-                    wa_codes[:, nb, g, :], wa_plane(nb, g),
-                )
+            if pair == 1:
+                later(QUANTISE_LAG, quantise_pass, nb, kind, g, now["grouped"])
+
+        def quantise_pass(nb, kind, g, grouped):
+            act_codes, act_planes = ((x_codes, x_planes), (h_codes, h_planes), (att_codes, att_planes))[kind]
+            kept = kind == 2 and nb < LATE_BLOCK
+            if kept:
+                if nb == EARLY_BLOCKS and g == 0:
+                    wa_codes.append(
+                        work.tile([P, LATE_BLOCK - EARLY_BLOCKS, H_PASSES, N_BLOCK], U32, tag="enc", name="wa_codes", align_bytes=64)
+                    )
+                codes, plane = wa_code(nb, g), wa_plane(nb, g)
+            else:
+                codes, plane = new_weight_operand(stage)
+            nc.vector.quantize_mx(out=codes.bitcast(FP8X4), scales=plane, in_=grouped[:])
+            if not kept:
+                later(MULTIPLY_LAG, add_product, nb, kind, g, (act_codes[:, g, :], act_planes[:, g, :], codes, plane))
+
+        def add_product(nb, kind, g, operands):
+            if kind == 0 and g == 0:
+                acc = psum.tile([P, N_BLOCK], F32, tag="acc", bufs=ACC_BANKS)
+                now["acc"] = acc
+            last_kind = 0 if nb == ATTN else 2 if nb >= LATE_BLOCK else 1
+            last = kind == last_kind and g == H_PASSES - 1
+            multiply(nc, now["acc"], [operands], start=(kind == 0 and g == 0), stop=last)
+            if last and nb == ATTN:
+                add_attn_bias(1, now["acc"])
+            elif last and nb >= LATE_BLOCK:
+                add_and_activate(nb % H_BLOCKS, 3, now["acc"])
+            elif last:
+                rows = slice(nb * N_BLOCK, (nb + 1) * N_BLOCK)
+                nc.vector.tensor_tensor(out=gates_xh[:, rows], in0=now["acc"][:], in1=gates_xh[:, rows], op=ALU.add)
 
         def lin_chunks(g):
             return attn_lin[:, g * K_PASS : (g + 1) * K_PASS].rearrange("b (t p) -> b t p", p=P)
 
-        def negated_peaks(g, part, neg_peak):
-            here = slice(part * PEAK_FEATS, (part + 1) * PEAK_FEATS)
-            enc = enc_passes[g][:, :, here]
-            there = slice(part * PEAK_FEATS // 4, (part + 1) * PEAK_FEATS // 4)
-            lin = lin_chunks(g)[:, :, there]
-            top = work.tile([P, QUARTER, PEAK_FEATS], BF16, tag="top", bufs=1)
-            low = work.tile([P, QUARTER, PEAK_FEATS], BF16, tag="low", bufs=1)
-            nc.vector.tensor_tensor(out=top[:], in0=enc[:, 0:QUARTER, :], in1=enc[:, QUARTER : 2 * QUARTER, :], op=ALU.max)
-            nc.vector.tensor_tensor(out=low[:], in0=enc[:, 0:QUARTER, :], in1=enc[:, QUARTER : 2 * QUARTER, :], op=ALU.min)
-            for i in range(2, S // QUARTER):
-                steps = slice(i * QUARTER, (i + 1) * QUARTER)
-                nc.vector.tensor_tensor(out=top[:], in0=top[:], in1=enc[:, steps, :], op=ALU.max)
-                nc.vector.tensor_tensor(out=low[:], in0=low[:], in1=enc[:, steps, :], op=ALU.min)
-            half = QUARTER // 2
-            while half >= 1:
-                nc.vector.tensor_tensor(out=top[:, 0:half, :], in0=top[:, 0:half, :], in1=top[:, half : 2 * half, :], op=ALU.max)
-                nc.vector.tensor_tensor(out=low[:, 0:half, :], in0=low[:, 0:half, :], in1=low[:, half : 2 * half, :], op=ALU.min)
-                half //= 2
-            neg_top = work.tile([P, 4, PEAK_FEATS // 4], F32, tag="neg_top", bufs=1)
-            neg_low = work.tile([P, 4, PEAK_FEATS // 4], F32, tag="neg_low", bufs=1)
-            for neg, extreme in ((neg_top, top), (neg_low, low)):
-                nc.vector.scalar_tensor_tensor(
-                    out=neg[:], in0=lin, scalar=-1.0, in1=extreme[:, 0, :].rearrange("b (p t) -> b t p", t=4),
-                    op0=ALU.mult, op1=ALU.mult,
+        def negated_peaks(g, part):
+            there = slice(part * PEAK_PART, (part + 1) * PEAK_PART)
+            feats = slice(4 * part * PEAK_PART, 4 * (part + 1) * PEAK_PART)
+            trees = []
+
+            def fold(i):
+                if i == 1:
+                    top = work.tile([P, FOLD, 4 * PEAK_PART], BF16, tag="top")
+                    low = work.tile([P, FOLD, 4 * PEAK_PART], BF16, tag="low")
+                    trees.extend([(top, ALU.max), (low, ALU.min)])
+                enc = enc_passes[g][:, :, feats]
+                for tree, op in trees:
+                    before = enc[:, 0:FOLD, :] if i == 1 else tree[:]
+                    nc.vector.tensor_tensor(out=tree[:], in0=before, in1=enc[:, i * FOLD : (i + 1) * FOLD, :], op=op)
+
+            def finish():
+                half = FOLD // 2
+                while half >= 1:
+                    for tree, op in trees:
+                        nc.vector.tensor_tensor(
+                            out=tree[:, 0:half, :], in0=tree[:, 0:half, :], in1=tree[:, half : 2 * half, :], op=op
+                        )
+                    half //= 2
+                ends = work.tile([P, 2, 4, PEAK_PART], F32, tag="terms", bufs=3)
+                for i, (tree, op) in enumerate(trees):
+                    nc.vector.scalar_tensor_tensor(
+                        out=ends[:, i, :, :], in0=lin_chunks(g)[:, :, there], scalar=-1.0,
+                        in1=tree[:, 0, :].rearrange("b (p t) -> b t p", t=4), op0=ALU.mult, op1=ALU.mult,
+                    )
+                nc.vector.tensor_tensor(
+                    out=neg_peaks[g][:, :, there], in0=ends[:, 0, :, :], in1=ends[:, 1, :, :], op=ALU.min
                 )
-            nc.vector.tensor_tensor(out=neg_peak[:, :, there], in0=neg_top[:], in1=neg_low[:], op=ALU.min)
+
+            return [(fold, (i,)) for i in range(1, S // FOLD)] + [(finish, ())]
 
         def chunk_of(g, t):
             return enc_passes[g][:].rearrange("b s (p t) -> b s t p", t=4)[:, :, t, :]
@@ -235,134 +299,262 @@ def tile_decoderlstm_pa_kernel(
                     start=(s == 0), stop=(s == S - 1),
                 )
 
-        def attention_by_scalar(g, t, neg_peak, mean):
-            enc = enc_passes[g]
-            enc_c = chunk_of(g, t)
-            exp_sum = work.tile([P, P], F32, tag="exp_sum")
-            exps = []
-            for half in range(P // SCALAR_PART):
-                exps_h = work.tile([P, SCALAR_PART, S], F32, tag="half_s", bufs=2)
-                for i in range(SCALAR_PART):
-                    p = half * SCALAR_PART + i
-                    j = 4 * p + t
-                    nc.scalar.activation(
-                        out=exps_h[:, i, :],
-                        in_=enc[:, :, j],
-                        func=ACT.Exp,
-                        scale=lin_chunks(g)[:, t, p : p + 1],
-                        bias=neg_peak[:, t, p : p + 1],
-                        accum_out=exp_sum[:, p : p + 1],
-                    )
-                exps.append(exps_h)
-            exp_total = psum.tile([P, P], F32, tag="sums", bufs=3)
-            nc.tensor.transpose(exp_total[:], exp_sum[:], ident[:])
-            inverse = work.tile([P, P], F32, tag="inverse")
-            nc.vector.reciprocal(out=inverse[:], in_=exp_total[:])
-            total = psum.tile([P, P], F32, tag="sums", bufs=3)
-            for part in range(HALVES):
-                steps = slice(part * S_HALF, (part + 1) * S_HALF)
-                terms = work.tile([P, S_HALF, P], F32, tag="half_v", bufs=3)
-                for half in range(P // SCALAR_PART):
-                    cols = slice(half * SCALAR_PART, (half + 1) * SCALAR_PART)
-                    nc.vector.tensor_tensor(
-                        out=terms[:, :, cols].rearrange("b (h l) p -> b h p l", l=2),
-                        in0=exps[half][:, :, steps].rearrange("b p (h l) -> b h p l", l=2),
-                        in1=enc_c[:, steps, cols].rearrange("b (h l) p -> b h p l", l=2),
-                        op=ALU.mult,
-                    )
-                sum_over_s(total, terms, part)
-            nc.vector.tensor_tensor(out=mean, in0=total[:], in1=inverse[:], op=ALU.mult)
-            return inverse
+        att_t = [work.tile([P, 4, P], F32, tag="att_t", name="att_t") for g in range(H_PASSES)]
+        chunks_left = [4] * H_PASSES
+        chunk = {}
 
-        def attention_by_vector(g, t, neg_peak, mean):
-            enc_c = chunk_of(g, t)
-            lin_c = lin_chunks(g)[:, t, :]
-            neg_peak_c = neg_peak[:, t, :]
-            exp_total = psum.tile([P, P], F32, tag="sums", bufs=3)
-            exps = []
-            for part in range(HALVES):
-                steps = slice(part * S_HALF, (part + 1) * S_HALF)
-                exps_h = work.tile([P, S_HALF, P], F32, tag="half_v", bufs=3)
-                nc.vector.tensor_tensor(
-                    out=exps_h[:], in0=enc_c[:, steps, :],
-                    in1=lin_c.unsqueeze(1).to_broadcast([P, S_HALF, P]), op=ALU.mult,
-                )
-                nc.vector.tensor_tensor(
-                    out=exps_h[:], in0=exps_h[:],
-                    in1=neg_peak_c.unsqueeze(1).to_broadcast([P, S_HALF, P]), op=ALU.add,
-                )
-                nc.scalar.activation(out=exps_h[:], in_=exps_h[:], func=ACT.Exp)
-                sum_over_s(exp_total, exps_h, part)
-                exps.append(exps_h)
-            inverse = work.tile([P, P], F32, tag="inverse")
-            nc.vector.reciprocal(out=inverse[:], in_=exp_total[:])
-            total = psum.tile([P, P], F32, tag="sums", bufs=3)
-            for part in range(HALVES):
-                steps = slice(part * S_HALF, (part + 1) * S_HALF)
-                terms = work.tile([P, S_HALF, P], F32, tag="half_v", bufs=3)
-                nc.vector.tensor_tensor(out=terms[:], in0=exps[part][:], in1=enc_c[:, steps, :], op=ALU.mult)
-                sum_over_s(total, terms, part)
-            nc.vector.tensor_tensor(out=mean, in0=total[:], in1=inverse[:], op=ALU.mult)
-            return inverse
-
-        neg_peaks = [work.tile([P, 4, P], F32, tag="neg_peak", name="neg_peak") for g in range(H_PASSES)]
-        for part in range(K_PASS // PEAK_FEATS):
-            negated_peaks(0, part, neg_peaks[0])
-        for c in range(CHUNKS):
+        def finish_chunk(c):
             g, t = divmod(c, 4)
-            if t == 0:
-                att_t = work.tile([P, 4, P], F32, tag="att_t", bufs=1)
-            block_words = load_gate_block(c)
-            if c == 0:
-                nc.sync.dma_start(out=gates_xh[:], in_=parked.partition_broadcast(P))
-            gate_block(c, *block_words)
-            if c == 0:
-                load_enc_steps(1, range(4))
-                nc.sync.dma_start(out=c_sb[:], in_=c_prev)
-            attention = attention_by_vector if c in VECTOR_CHUNKS else attention_by_scalar
-            inverse = attention(g, t, neg_peaks[g], att_t[:, t, :])
-            if c in (1, 2):
-                negated_peaks(1, c - 1, neg_peaks[1])
-            if t == 3:
-                att_grouped = work.tile([P, P, 4], BF16, tag="att_grouped", bufs=1, align_bytes=64)
-                nc.vector.tensor_copy(out=att_grouped[:], in_=att_t[:].rearrange("p t b -> p b t"))
+            nc.vector.tensor_tensor(out=att_t[g][:, t, :], in0=chunk[c, "total"][:], in1=chunk[c, "inverse"][:], op=ALU.mult)
+            chunks_left[g] -= 1
+            if chunks_left[g] == 0:
+                att_grouped = stage.tile([P, P, 4], BF16, tag="grouped", bufs=3, align_bytes=64)
+                nc.vector.tensor_copy(out=att_grouped[:], in_=att_t[g][:].rearrange("p t b -> p b t"))
                 nc.vector.quantize_mx(
                     out=att_codes[:, g, :].bitcast(FP8X4),
                     scales=att_planes[:, g, :],
                     in_=att_grouped[:].rearrange("p b t -> p (b t)"),
                 )
 
-        warm = work.tile([P, 1], F32, tag="warm", bufs=1)
-        nc.scalar.activation(out=warm[:], in_=inverse[:, 0:1], func=ACT.Sigmoid)
+        def new_sum():
+            total = psum.tile([P, P], F32, tag="sums", bufs=SUM_BANKS)
+            return total
 
-        for part in range(H_BLOCKS):
-            cols = slice(part * N_BLOCK, (part + 1) * N_BLOCK)
-            cell = work.tile([P, 8, N_BLOCK], F32, tag="enc")
-            for gate in range(4):
-                nb = gate * H_BLOCKS + part
-                acc = psum.tile([P, N_BLOCK], F32, tag="acc")
-                for g in range(H_PASSES):
-                    nc.tensor.matmul_mx(
-                        out=acc[:],
-                        lhsT=att_codes[:, g, :].bitcast(FP8X4),
-                        lhsT_scale=att_planes[:, g, :],
-                        rhs=wa_codes[:, nb, g, :].bitcast(FP8X4),
-                        rhs_scale=wa_plane(nb, g),
-                        start=(g == 0),
-                        stop=(g == H_PASSES - 1),
-                    )
-                nc.vector.tensor_tensor(
-                    out=cell[:, gate, :], in0=acc[:], in1=gates_xh[:, nb * N_BLOCK : (nb + 1) * N_BLOCK], op=ALU.add
-                )
+        def invert_sum(c, exp_total):
+            inverse = work.tile([P, P], F32, tag="inverse")
+            nc.vector.reciprocal(out=inverse[:], in_=exp_total[:])
+            chunk[c, "inverse"] = inverse
+
+        def scalar_step(step):
+            at, i = divmod(step, P // ACTS_A_STEP)
+            c = SCALAR_CHUNKS[at]
+            g, t = divmod(c, 4)
+            half, row = divmod(i * ACTS_A_STEP, SCALAR_PART)
+            if i == 0:
+                exp_sum = work.tile([P, P], F32, tag="exp_sum")
+                chunk[c, "exp_sum"] = exp_sum
+                chunk[c, "terms"] = []
+            if row == 0:
+                exps = work.tile([P, SCALAR_PART, S], F32, tag="exps_s", bufs=2)
+                chunk[c, "exps"] = exps
+            exps, exp_sum = chunk[c, "exps"], chunk[c, "exp_sum"]
+            for k in range(row, row + ACTS_A_STEP):
+                p = half * SCALAR_PART + k
                 nc.scalar.activation(
-                    out=cell[:, gate, :], in_=cell[:, gate, :], func=(ACT.Tanh if gate == 2 else ACT.Sigmoid)
+                    out=exps[:, k, :],
+                    in_=enc_passes[g][:, :, 4 * p + t],
+                    func=ACT.Exp,
+                    scale=lin_chunks(g)[:, t, p : p + 1],
+                    bias=neg_peaks[g][:, t, p : p + 1],
+                    accum_out=exp_sum[:, p : p + 1],
                 )
-            gate_i, gate_f, gate_g, gate_o = [cell[:, gate, :] for gate in range(4)]
-            kept, c_new, tanh_c, h_new = [cell[:, 4 + i, :] for i in range(4)]
-            nc.vector.tensor_tensor(out=kept, in0=gate_f, in1=c_sb[:, cols], op=ALU.mult)
+            if row + ACTS_A_STEP < SCALAR_PART:
+                return
+            cols = slice(half * SCALAR_PART, (half + 1) * SCALAR_PART)
+            for part in range(HALVES):
+                steps = slice(part * S_HALF, (part + 1) * S_HALF)
+                if half == 0:
+                    terms = work.tile([P, S_HALF, P], F32, tag="terms", bufs=3)
+                    chunk[c, "terms"].append(terms)
+                nc.vector.tensor_tensor(
+                    out=chunk[c, "terms"][part][:, :, cols].rearrange("b (h l) p -> b h p l", l=2),
+                    in0=exps[:, :, steps].rearrange("b p (h l) -> b h p l", l=2),
+                    in1=chunk_of(g, t)[:, steps, cols].rearrange("b (h l) p -> b h p l", l=2),
+                    op=ALU.mult,
+                )
+            if half == 0:
+                return
+            later(1, turn_exp_sum, c)
+            later(SUM_LAG, sum_scalar_chunk, c)
+
+        def turn_exp_sum(c):
+            exp_total = new_sum()
+            nc.tensor.transpose(exp_total[:], chunk[c, "exp_sum"][:], ident[:])
+            invert_sum(c, exp_total)
+
+        def sum_scalar_chunk(c):
+            total = new_sum()
+            for part in range(HALVES):
+                sum_over_s(total, chunk[c, "terms"][part], part)
+            chunk[c, "total"] = total
+            finish_chunk(c)
+
+        def vector_scores(c, part):
+            g, t = divmod(c, 4)
+            exps = work.tile([P, S_HALF, P], F32, tag="exps_v", bufs=2)
+            nc.vector.tensor_tensor(
+                out=exps[:], in0=chunk_of(g, t)[:, part * S_HALF : (part + 1) * S_HALF, :],
+                in1=lin_chunks(g)[:, t, :].unsqueeze(1).to_broadcast([P, S_HALF, P]), op=ALU.mult,
+            )
+            chunk[c, part] = exps
+
+        def vector_exps(c, part):
+            g, t = divmod(c, 4)
+            exps = chunk[c, part]
+            nc.vector.tensor_tensor(
+                out=exps[:], in0=exps[:],
+                in1=neg_peaks[g][:, t, :].unsqueeze(1).to_broadcast([P, S_HALF, P]), op=ALU.add,
+            )
+            later(EXP_LAG, exp_vector_scores, c, part)
+
+        def exp_vector_scores(c, part):
+            exps = chunk[c, part]
+            nc.scalar.activation(out=exps[:], in_=exps[:], func=ACT.Exp)
+            later(EXP_LAG, sum_vector_exps, c, part)
+
+        def sum_vector_exps(c, part):
+            if part == 0:
+                chunk[c, "exp_total"] = new_sum()
+            sum_over_s(chunk[c, "exp_total"], chunk[c, part], part)
+            if part == HALVES - 1:
+                invert_sum(c, chunk[c, "exp_total"])
+            vector_terms(c, part)
+
+        def vector_terms(c, part):
+            g, t = divmod(c, 4)
+            terms = work.tile([P, S_HALF, P], F32, tag="terms", bufs=3)
+            nc.vector.tensor_tensor(
+                out=terms[:], in0=chunk[c, part][:], in1=chunk_of(g, t)[:, part * S_HALF : (part + 1) * S_HALF, :], op=ALU.mult
+            )
+            chunk[c, "terms", part] = terms
+            later(SUM_LAG, sum_vector_terms, c, part)
+
+        def sum_vector_terms(c, part):
+            if part == 0:
+                chunk[c, "total"] = new_sum()
+            sum_over_s(chunk[c, "total"], chunk[c, "terms", part], part)
+            if part == HALVES - 1:
+                finish_chunk(c)
+
+        def add_and_activate(part, i, acc):
+            value = cells[0][:, part, i, :]
+            nb = i * H_BLOCKS + part
+            nc.vector.tensor_tensor(out=value, in0=acc[:], in1=gates_xh[:, nb * N_BLOCK : (nb + 1) * N_BLOCK], op=ALU.add)
+            later(ACT_LAG, activate, value, ACT.Tanh if i == 2 else ACT.Sigmoid)
+
+        def activate(value, func):
+            nc.scalar.activation(out=value, in_=value, func=func)
+
+        def gate(part, i):
+            nb = i * H_BLOCKS + part
+            acc = psum.tile([P, N_BLOCK], F32, tag="sums", bufs=SUM_BANKS)
+            multiply(nc, acc, [(att_codes[:, g, :], att_planes[:, g, :], wa_code(nb, g), wa_plane(nb, g)) for g in range(H_PASSES)])
+            add_and_activate(part, i, acc)
+
+        def new_cell_state(part):
+            cols = slice(part * N_BLOCK, (part + 1) * N_BLOCK)
+            gate_i, gate_f, gate_g = [cells[0][:, part, i, :] for i in range(3)]
+            kept, c_new, tanh_c = [cells[0][:, part, i, :] for i in range(4, 7)]
+            nc.vector.tensor_tensor(out=kept, in0=gate_f, in1=now["c"][:, cols], op=ALU.mult)
             nc.vector.tensor_tensor(out=c_new, in0=gate_i, in1=gate_g, op=ALU.mult)
             nc.vector.tensor_tensor(out=c_new, in0=c_new, in1=kept, op=ALU.add)
             nc.sync.dma_start(out=out_1[:, cols], in_=c_new)
+            later(ACT_LAG, activate_into, tanh_c, c_new)
+
+        def activate_into(tanh_c, c_new):
             nc.scalar.activation(out=tanh_c, in_=c_new, func=ACT.Tanh)
-            nc.vector.tensor_tensor(out=h_new, in0=gate_o, in1=tanh_c, op=ALU.mult)
-            nc.sync.dma_start(out=out_0[:, cols], in_=h_new)
+
+        def new_hidden_state(part):
+            h_new = cells[0][:, part, 7, :]
+            nc.vector.tensor_tensor(out=h_new, in0=cells[0][:, part, 3, :], in1=cells[0][:, part, 6, :], op=ALU.mult)
+            nc.sync.dma_start(out=out_0[:, part * N_BLOCK : (part + 1) * N_BLOCK], in_=h_new)
+
+        def later(lag, step, *args):
+            waiting.append((now["half passes"] + lag, step, args))
+
+        def run_waiting(upto):
+            due = [entry for entry in waiting if entry[0] <= upto]
+            for entry in due:
+                waiting.remove(entry)
+            for at, step, args in due:
+                step(*args)
+
+        def merge(streams):
+            taken = [0] * len(streams)
+            for w, half_pass in enumerate(half_passes):
+                now["half passes"] = w
+                run_waiting(w)
+                for i, (first, last, steps) in enumerate(streams):
+                    upto = min(len(steps), max(0, -(-(w + 1 - first) * len(steps) // (last - first))))
+                    for step, args in steps[taken[i] : upto]:
+                        step(*args)
+                    taken[i] = upto
+                weight_step(*half_pass)
+            while waiting:
+                now["half passes"] = min(entry[0] for entry in waiting)
+                run_waiting(now["half passes"])
+
+        neg_peaks = [work.tile([P, 4, P], F32, tag="neg_peak", name="neg_peak") for g in range(H_PASSES)]
+        peak_parts = [negated_peaks(0, part) for part in range(2)]
+        peak_steps = [step for pair in zip(*peak_parts) for step in pair[:2]][: 2 * FOLDS_IN_TURN]
+        for steps in peak_parts:
+            peak_steps.extend(steps[FOLDS_IN_TURN:])
+        peaks_taken = []
+
+        def first_peak_steps(n):
+            for step, args in peak_steps[len(peaks_taken) : len(peaks_taken) + n]:
+                step(*args)
+                peaks_taken.append(step)
+
+        def run_both(first, second):
+            for step, args in (first, second):
+                step(*args)
+
+        vector_stream = []
+        for c in VECTOR_CHUNKS:
+            if c == VECTOR_CHUNKS[1]:
+                vector_stream.extend([(run_both, pair) for pair in zip(negated_peaks(1, 0), negated_peaks(1, 1))])
+            for step in (vector_scores, vector_exps):
+                vector_stream.extend([(step, (c, part)) for part in range(HALVES)])
+            if c == VECTOR_CHUNKS[1]:
+                vector_stream.append((load_c, ()))
+        half_passes = []
+        for nb in range(GATE_BLOCKS):
+            if nb == 1:
+                half_passes.extend([(ATTN, 0, g, pair) for g in range(H_PASSES) for pair in range(2)])
+            half_passes.extend([(nb, kind, g, pair) for kind in range(3) for g in range(H_PASSES) for pair in range(2)])
+        scalar_stream = [(scalar_step, (i,)) for i in range(len(SCALAR_CHUNKS) * P // ACTS_A_STEP)]
+
+        def start_cell():
+            warm = work.tile([P, 1], F32, tag="warm", bufs=1)
+            nc.scalar.activation(out=warm[:], in_=ident[:, 0:1], func=ACT.Sigmoid)
+            cells.append(work.tile([P, H_BLOCKS, 8, N_BLOCK], F32, tag="enc", name="cells", align_bytes=64))
+
+        cells = []
+        cell_stream = [(start_cell, ())]
+        for part in range(H_BLOCKS):
+            cell_stream.extend([(gate, (part, i)) for i in range(4) if i * H_BLOCKS + part < LATE_BLOCK])
+            cell_stream.append((later, (ACT_LAG, new_cell_state, part)))
+        cell_stream.extend([(later, (2 * ACT_LAG + 1, new_hidden_state, part)) for part in range(H_BLOCKS - 1)])
+        with tc.manual_schedule(engines={mybir.EngineType.Activation, mybir.EngineType.PE, mybir.EngineType.DVE}):
+            x_turned = turn_activations(nc, psum, stage, ident, x_sb)
+            h_sb = stage.tile([P, H], BF16, tag="act_rows", bufs=2)
+            nc.sync.dma_start(out=h_sb[:], in_=h_prev)
+            load_enc_steps(0, range(3, 4))
+            first_peak_steps(2)
+            quantise_activations(nc, x_turned, x_codes, x_planes)
+            first_peak_steps(2 * FOLDS_IN_TURN - 2)
+            passes = []
+            for g in range(H_PASSES):
+                grouped = new_grouped(stage)
+                for pair in range(2):
+                    transpose_half(nc, psum, ident, attn_words[:, :, g * PASS_WORDS : (g + 1) * PASS_WORDS], pair, grouped)
+                codes, plane = new_weight_operand(stage)
+                nc.vector.quantize_mx(out=codes.bitcast(FP8X4), scales=plane, in_=grouped[:])
+                passes.append((x_codes[:, g, :], x_planes[:, g, :], codes, plane))
+            h_turned = turn_activations(nc, psum, stage, ident, h_sb)
+            acc = psum.tile([P, N_BLOCK], F32, tag="acc", bufs=ACC_BANKS)
+            multiply(nc, acc, passes)
+            first_peak_steps(2)
+            add_attn_bias(0, acc)
+            first_peak_steps(1)
+            quantise_activations(nc, h_turned, h_codes, h_planes)
+            merge(
+                (
+                    (0, PEAKS_END, peak_steps[len(peaks_taken) :]),
+                    (SCALAR_START, SCALAR_END, scalar_stream),
+                    (PEAKS_END, VECTOR_END, vector_stream),
+                    (CELL_START, len(half_passes), cell_stream),
+                )
+            )
+            new_hidden_state(H_BLOCKS - 1)

@@ -25,6 +25,8 @@ LATE_BLOCK = 7
 EARLY_BLOCKS = 4
 ATTN = -1
 ENC_LOADS = {0: range(0, 1), 1: range(1, 4)}
+TERM_BUFS = 4
+CODE_BUFS = 5
 ACC_BANKS = 1
 TURN_BANKS = 3
 SUM_BANKS = 4
@@ -37,11 +39,12 @@ SCALAR_START = 2
 FOLDS_IN_TURN = 5
 PEAKS_END = 6
 SCALAR_END = 88
-VECTOR_END = 76
+VECTOR_END = 78
 CELL_START = 92
 ACT_LAG = 1
 QUANTISE_LAG = 2
 MULTIPLY_LAG = 4
+SUM_PIECE = 8
 SUM_LAG = 3
 EXP_LAG = 3
 QUARTER = S // 4
@@ -54,7 +57,7 @@ FLOPS = 2 * P * (H * H + 4 * H * 3 * H)
 
 
 def load_weight_rows(nc, stage, rows, order="(t p) k -> p t k"):
-    w_rows = stage.tile([P, ROW_TILES, H], BF16, tag="w_rows", bufs=4)
+    w_rows = stage.tile([P, ROW_TILES, H], BF16, tag="w_rows", bufs=3)
     nc.sync.dma_start(out=w_rows[:], in_=rows.rearrange(order, p=P))
     return w_rows[:].bitcast(F32)
 
@@ -65,8 +68,8 @@ def new_grouped(stage):
 
 
 def new_weight_operand(stage):
-    codes = stage.tile([P, N_BLOCK], U32, tag="w_codes", bufs=4, align_bytes=64)
-    plane = stage.tile([P, N_BLOCK], U8, tag="w_plane", bufs=4, align_bytes=64)
+    codes = stage.tile([P, N_BLOCK], U32, tag="w_codes", bufs=CODE_BUFS, align_bytes=64)
+    plane = stage.tile([P, N_BLOCK], U8, tag="w_plane", bufs=CODE_BUFS, align_bytes=64)
     return codes[:], plane[:]
 
 
@@ -147,11 +150,11 @@ def tile_decoderlstm_pa_kernel(
         nc.scalar.activation(out=warm_exp[:], in_=ident[:, 0:1], func=ACT.Exp)
 
         enc_passes = []
-        x_sb = stage.tile([P, H], BF16, tag="act_rows", bufs=2)
+        x_sb = stage.tile([P, H], BF16, tag="grouped", bufs=3, align_bytes=64)
         nc.sync.dma_start(out=x_sb[:], in_=x)
         load_enc_steps(0, range(3))
         attn_words = load_attn_rows(0)
-        attn_b_all = stage.tile([P, H], BF16, tag="act_rows", bufs=2)
+        attn_b_all = stage.tile([P, H], BF16, tag="attn_b", bufs=1)
         nc.sync.dma_start(out=attn_b_all[:], in_=attn_b.partition_broadcast(P))
 
         biases = [work.tile([P, 4 * H // P], BF16, tag="bias", name="bias") for i in range(2)]
@@ -180,7 +183,7 @@ def tile_decoderlstm_pa_kernel(
             )
 
         def load_c():
-            c_sb = stage.tile([P, H], BF16, tag="act_rows", bufs=2)
+            c_sb = work.tile([P, H], BF16, tag="exps_v", bufs=2)
             nc.sync.dma_start(out=c_sb[:], in_=c_prev)
             now["c"] = c_sb
 
@@ -202,7 +205,7 @@ def tile_decoderlstm_pa_kernel(
             rows = slice(nb * N_BLOCK, (nb + 1) * N_BLOCK)
             return [load_weight_rows(nc, stage, w) for w in (W_ih0[rows, 0:H], W_hh0[rows, :], W_ih0[rows, H : 2 * H])]
 
-        now = {}
+        now = {"passes": []}
         waiting = []
 
         def weight_step(nb, kind, g, pair):
@@ -232,16 +235,19 @@ def tile_decoderlstm_pa_kernel(
             else:
                 codes, plane = new_weight_operand(stage)
             nc.vector.quantize_mx(out=codes.bitcast(FP8X4), scales=plane, in_=grouped[:])
-            if not kept:
-                later(MULTIPLY_LAG, add_product, nb, kind, g, (act_codes[:, g, :], act_planes[:, g, :], codes, plane))
+            if kept:
+                return
+            now["passes"].append((act_codes[:, g, :], act_planes[:, g, :], codes, plane))
+            if (kind, g) in ((2, 1), (0 if nb == ATTN else 1, 1)):
+                later(MULTIPLY_LAG, add_products, nb, kind, now["passes"])
+                now["passes"] = []
 
-        def add_product(nb, kind, g, operands):
-            if kind == 0 and g == 0:
+        def add_products(nb, kind, passes):
+            if kind < 2:
                 acc = psum.tile([P, N_BLOCK], F32, tag="acc", bufs=ACC_BANKS)
                 now["acc"] = acc
-            last_kind = 0 if nb == ATTN else 2 if nb >= LATE_BLOCK else 1
-            last = kind == last_kind and g == H_PASSES - 1
-            multiply(nc, now["acc"], [operands], start=(kind == 0 and g == 0), stop=last)
+            last = kind == 2 or nb < LATE_BLOCK
+            multiply(nc, now["acc"], passes, start=(kind < 2), stop=last)
             if last and nb == ATTN:
                 add_attn_bias(1, now["acc"])
             elif last and nb >= LATE_BLOCK:
@@ -276,7 +282,7 @@ def tile_decoderlstm_pa_kernel(
                             out=tree[:, 0:half, :], in0=tree[:, 0:half, :], in1=tree[:, half : 2 * half, :], op=op
                         )
                     half //= 2
-                ends = work.tile([P, 2, 4, PEAK_PART], F32, tag="terms", bufs=3)
+                ends = work.tile([P, 2, 4, PEAK_PART], F32, tag="terms", bufs=TERM_BUFS)
                 for i, (tree, op) in enumerate(trees):
                     nc.vector.scalar_tensor_tensor(
                         out=ends[:, i, :, :], in0=lin_chunks(g)[:, :, there], scalar=-1.0,
@@ -291,13 +297,21 @@ def tile_decoderlstm_pa_kernel(
         def chunk_of(g, t):
             return enc_passes[g][:].rearrange("b s (p t) -> b s t p", t=4)[:, :, t, :]
 
-        def sum_over_s(total, tiles, part):
-            for i in range(S_HALF):
+        def add_positions(c, name, tiles, part, first, behind):
+            if part == 0 and first == 0:
+                total = psum.tile([P, P], F32, tag="sums", bufs=SUM_BANKS)
+                chunk[c, name] = total
+            for i in range(first, first + SUM_PIECE):
                 s = part * S_HALF + i
                 nc.tensor.matmul(
-                    out=total[:], lhsT=tiles[:, i, :], rhs=ident[:], is_transpose=True,
+                    out=chunk[c, name][:], lhsT=tiles[:, i, :], rhs=ident[:], is_transpose=True,
                     start=(s == 0), stop=(s == S - 1),
                 )
+            if first + SUM_PIECE < S_HALF:
+                later(1, add_positions, c, name, tiles, part, first + SUM_PIECE, behind)
+            elif behind:
+                step, args = behind
+                step(*args)
 
         att_t = [work.tile([P, 4, P], F32, tag="att_t", name="att_t") for g in range(H_PASSES)]
         chunks_left = [4] * H_PASSES
@@ -316,11 +330,8 @@ def tile_decoderlstm_pa_kernel(
                     in_=att_grouped[:].rearrange("p b t -> p (b t)"),
                 )
 
-        def new_sum():
-            total = psum.tile([P, P], F32, tag="sums", bufs=SUM_BANKS)
-            return total
-
-        def invert_sum(c, exp_total):
+        def invert_sum(c):
+            exp_total = chunk[c, "exp_total"]
             inverse = work.tile([P, P], F32, tag="inverse")
             nc.vector.reciprocal(out=inverse[:], in_=exp_total[:])
             chunk[c, "inverse"] = inverse
@@ -354,7 +365,7 @@ def tile_decoderlstm_pa_kernel(
             for part in range(HALVES):
                 steps = slice(part * S_HALF, (part + 1) * S_HALF)
                 if half == 0:
-                    terms = work.tile([P, S_HALF, P], F32, tag="terms", bufs=3)
+                    terms = work.tile([P, S_HALF, P], F32, tag="terms", bufs=TERM_BUFS)
                     chunk[c, "terms"].append(terms)
                 nc.vector.tensor_tensor(
                     out=chunk[c, "terms"][part][:, :, cols].rearrange("b (h l) p -> b h p l", l=2),
@@ -368,16 +379,15 @@ def tile_decoderlstm_pa_kernel(
             later(SUM_LAG, sum_scalar_chunk, c)
 
         def turn_exp_sum(c):
-            exp_total = new_sum()
+            exp_total = psum.tile([P, P], F32, tag="sums", bufs=SUM_BANKS)
             nc.tensor.transpose(exp_total[:], chunk[c, "exp_sum"][:], ident[:])
-            invert_sum(c, exp_total)
+            chunk[c, "exp_total"] = exp_total
+            invert_sum(c)
 
         def sum_scalar_chunk(c):
-            total = new_sum()
-            for part in range(HALVES):
-                sum_over_s(total, chunk[c, "terms"][part], part)
-            chunk[c, "total"] = total
-            finish_chunk(c)
+            terms = chunk[c, "terms"]
+            second = (add_positions, (c, "total", terms[1], 1, 0, (finish_chunk, (c,))))
+            add_positions(c, "total", terms[0], 0, 0, (later, (1,) + second[:1] + second[1]))
 
         def vector_scores(c, part):
             g, t = divmod(c, 4)
@@ -403,16 +413,13 @@ def tile_decoderlstm_pa_kernel(
             later(EXP_LAG, sum_vector_exps, c, part)
 
         def sum_vector_exps(c, part):
-            if part == 0:
-                chunk[c, "exp_total"] = new_sum()
-            sum_over_s(chunk[c, "exp_total"], chunk[c, part], part)
-            if part == HALVES - 1:
-                invert_sum(c, chunk[c, "exp_total"])
+            behind = (invert_sum, (c,)) if part == HALVES - 1 else None
+            add_positions(c, "exp_total", chunk[c, part], part, 0, behind)
             vector_terms(c, part)
 
         def vector_terms(c, part):
             g, t = divmod(c, 4)
-            terms = work.tile([P, S_HALF, P], F32, tag="terms", bufs=3)
+            terms = work.tile([P, S_HALF, P], F32, tag="terms", bufs=TERM_BUFS)
             nc.vector.tensor_tensor(
                 out=terms[:], in0=chunk[c, part][:], in1=chunk_of(g, t)[:, part * S_HALF : (part + 1) * S_HALF, :], op=ALU.mult
             )
@@ -420,11 +427,8 @@ def tile_decoderlstm_pa_kernel(
             later(SUM_LAG, sum_vector_terms, c, part)
 
         def sum_vector_terms(c, part):
-            if part == 0:
-                chunk[c, "total"] = new_sum()
-            sum_over_s(chunk[c, "total"], chunk[c, "terms", part], part)
-            if part == HALVES - 1:
-                finish_chunk(c)
+            behind = (finish_chunk, (c,)) if part == HALVES - 1 else None
+            add_positions(c, "total", chunk[c, "terms", part], part, 0, behind)
 
         def add_and_activate(part, i, acc):
             value = cells[0][:, part, i, :]
@@ -506,8 +510,6 @@ def tile_decoderlstm_pa_kernel(
                 vector_stream.extend([(run_both, pair) for pair in zip(negated_peaks(1, 0), negated_peaks(1, 1))])
             for step in (vector_scores, vector_exps):
                 vector_stream.extend([(step, (c, part)) for part in range(HALVES)])
-            if c == VECTOR_CHUNKS[1]:
-                vector_stream.append((load_c, ()))
         half_passes = []
         for nb in range(GATE_BLOCKS):
             if nb == 1:
@@ -521,14 +523,14 @@ def tile_decoderlstm_pa_kernel(
             cells.append(work.tile([P, H_BLOCKS, 8, N_BLOCK], F32, tag="enc", name="cells", align_bytes=64))
 
         cells = []
-        cell_stream = [(start_cell, ())]
+        cell_stream = [(load_c, ()), (start_cell, ())]
         for part in range(H_BLOCKS):
             cell_stream.extend([(gate, (part, i)) for i in range(4) if i * H_BLOCKS + part < LATE_BLOCK])
             cell_stream.append((later, (ACT_LAG, new_cell_state, part)))
         cell_stream.extend([(later, (2 * ACT_LAG + 1, new_hidden_state, part)) for part in range(H_BLOCKS - 1)])
         with tc.manual_schedule(engines={mybir.EngineType.Activation, mybir.EngineType.PE, mybir.EngineType.DVE}):
             x_turned = turn_activations(nc, psum, stage, ident, x_sb)
-            h_sb = stage.tile([P, H], BF16, tag="act_rows", bufs=2)
+            h_sb = stage.tile([P, H], BF16, tag="grouped", bufs=3, align_bytes=64)
             nc.sync.dma_start(out=h_sb[:], in_=h_prev)
             load_enc_steps(0, range(3, 4))
             first_peak_steps(2)

@@ -28,17 +28,19 @@ ENC_LOADS = {0: range(0, 1), 1: range(1, 4)}
 TERM_BUFS = 4
 CODE_BUFS = 5
 ACC_BANKS = 1
-TURN_BANKS = 3
-SUM_BANKS = 4
+TURN_BANKS = 4
+SUM_BANKS = 3
 CHUNKS = 8
 SCALAR_PART = P // 2
 VECTOR_CHUNKS = (2, 4, 6)
 SCALAR_CHUNKS = (0, 1, 3, 5, 7)
 ACTS_A_STEP = 8
-SCALAR_START = 2
-FOLDS_IN_TURN = 5
+SCALAR_START = 4
+FIRST_ACTS = 6
+FIRST_PEAKS = 4
+FOLDS_BEHIND = 3
 PEAKS_END = 6
-SCALAR_END = 88
+SCALAR_END = 86
 VECTOR_END = 78
 CELL_START = 92
 ACT_LAG = 1
@@ -133,13 +135,14 @@ def tile_decoderlstm_pa_kernel(
         work = stack.enter_context(tc.tile_pool(name="work", bufs=2))
         psum = stack.enter_context(tc.psum_pool(name="psum", bufs=2))
 
-        def load_enc_steps(g, quarters):
+        def load_enc_steps(g, quarters, part=None):
             if len(enc_passes) == g:
                 enc_passes.append(work.tile([P, S, K_PASS], BF16, tag="enc", name="enc", align_bytes=64))
-            feats = slice(g * K_PASS, (g + 1) * K_PASS)
+            here = slice(0, K_PASS) if part is None else slice(4 * part * PEAK_PART, 4 * (part + 1) * PEAK_PART)
+            feats = slice(g * K_PASS + here.start, g * K_PASS + here.stop)
             for i in quarters:
                 steps = slice(i * QUARTER, (i + 1) * QUARTER)
-                nc.sync.dma_start(out=enc_passes[g][:, steps, :], in_=enc_seq[steps, :, feats].rearrange("s b j -> b s j"))
+                nc.sync.dma_start(out=enc_passes[g][:, steps, here], in_=enc_seq[steps, :, feats].rearrange("s b j -> b s j"))
 
         def load_attn_rows(nb):
             return load_weight_rows(nc, stage, attn_W[nb * N_BLOCK : (nb + 1) * N_BLOCK, :], "(p t) k -> p t k")
@@ -152,7 +155,7 @@ def tile_decoderlstm_pa_kernel(
         enc_passes = []
         x_sb = stage.tile([P, H], BF16, tag="grouped", bufs=3, align_bytes=64)
         nc.sync.dma_start(out=x_sb[:], in_=x)
-        load_enc_steps(0, range(3))
+        load_enc_steps(0, range(4), 0)
         attn_words = load_attn_rows(0)
         attn_b_all = stage.tile([P, H], BF16, tag="attn_b", bufs=1)
         nc.sync.dma_start(out=attn_b_all[:], in_=attn_b.partition_broadcast(P))
@@ -489,10 +492,7 @@ def tile_decoderlstm_pa_kernel(
                 run_waiting(now["half passes"])
 
         neg_peaks = [work.tile([P, 4, P], F32, tag="neg_peak", name="neg_peak") for g in range(H_PASSES)]
-        peak_parts = [negated_peaks(0, part) for part in range(2)]
-        peak_steps = [step for pair in zip(*peak_parts) for step in pair[:2]][: 2 * FOLDS_IN_TURN]
-        for steps in peak_parts:
-            peak_steps.extend(steps[FOLDS_IN_TURN:])
+        peak_steps = negated_peaks(0, 0) + negated_peaks(0, 1)
         peaks_taken = []
 
         def first_peak_steps(n):
@@ -532,10 +532,10 @@ def tile_decoderlstm_pa_kernel(
             x_turned = turn_activations(nc, psum, stage, ident, x_sb)
             h_sb = stage.tile([P, H], BF16, tag="grouped", bufs=3, align_bytes=64)
             nc.sync.dma_start(out=h_sb[:], in_=h_prev)
-            load_enc_steps(0, range(3, 4))
-            first_peak_steps(2)
+            load_enc_steps(0, range(4), 1)
+            first_peak_steps(1)
             quantise_activations(nc, x_turned, x_codes, x_planes)
-            first_peak_steps(2 * FOLDS_IN_TURN - 2)
+            first_peak_steps(S // FOLD - 2)
             passes = []
             for g in range(H_PASSES):
                 grouped = new_grouped(stage)
@@ -547,14 +547,18 @@ def tile_decoderlstm_pa_kernel(
             h_turned = turn_activations(nc, psum, stage, ident, h_sb)
             acc = psum.tile([P, N_BLOCK], F32, tag="acc", bufs=ACC_BANKS)
             multiply(nc, acc, passes)
-            first_peak_steps(2)
             add_attn_bias(0, acc)
             first_peak_steps(1)
+            first_peak_steps(FOLDS_BEHIND)
             quantise_activations(nc, h_turned, h_codes, h_planes)
+            now["half passes"] = 0
+            for step, args in scalar_stream[:FIRST_ACTS]:
+                step(*args)
+            first_peak_steps(FIRST_PEAKS)
             merge(
                 (
                     (0, PEAKS_END, peak_steps[len(peaks_taken) :]),
-                    (SCALAR_START, SCALAR_END, scalar_stream),
+                    (SCALAR_START, SCALAR_END, scalar_stream[FIRST_ACTS:]),
                     (PEAKS_END, VECTOR_END, vector_stream),
                     (CELL_START, len(half_passes), cell_stream),
                 )

@@ -45,8 +45,10 @@ VECTOR_END = 78
 CELL_START = 92
 ACT_LAG = 1
 QUANTISE_LAG = 2
-MULTIPLY_LAG = 4
+MULTIPLY_LAG = 3
 SUM_PIECE = 8
+TURN_LAG = 2
+TERM_LAG = 1
 SUM_LAG = 3
 EXP_LAG = 3
 QUARTER = S // 4
@@ -262,40 +264,46 @@ def tile_decoderlstm_pa_kernel(
         def lin_chunks(g):
             return attn_lin[:, g * K_PASS : (g + 1) * K_PASS].rearrange("b (t p) -> b t p", p=P)
 
-        def negated_peaks(g, part):
-            there = slice(part * PEAK_PART, (part + 1) * PEAK_PART)
-            feats = slice(4 * part * PEAK_PART, 4 * (part + 1) * PEAK_PART)
+        def negated_peaks(g):
             trees = []
 
-            def fold(i):
-                if i == 1:
-                    top = work.tile([P, FOLD, 4 * PEAK_PART], BF16, tag="top")
-                    low = work.tile([P, FOLD, 4 * PEAK_PART], BF16, tag="low")
-                    trees.extend([(top, ALU.max), (low, ALU.min)])
-                enc = enc_passes[g][:, :, feats]
-                for tree, op in trees:
-                    before = enc[:, 0:FOLD, :] if i == 1 else tree[:]
-                    nc.vector.tensor_tensor(out=tree[:], in0=before, in1=enc[:, i * FOLD : (i + 1) * FOLD, :], op=op)
+            def feats(part):
+                return slice(0, K_PASS) if part is None else slice(4 * part * PEAK_PART, 4 * (part + 1) * PEAK_PART)
 
-            def finish():
+            def fold(i, part):
+                if not trees:
+                    top = work.tile([P, FOLD, K_PASS], BF16, tag="top", bufs=1)
+                    low = work.tile([P, FOLD, K_PASS], BF16, tag="low", bufs=1)
+                    trees.extend([(top, ALU.max), (low, ALU.min)])
+                here = feats(part)
+                enc = enc_passes[g][:, :, here]
+                for tree, op in trees:
+                    before = enc[:, 0:FOLD, :] if i == 1 else tree[:, :, here]
+                    nc.vector.tensor_tensor(
+                        out=tree[:, :, here], in0=before, in1=enc[:, i * FOLD : (i + 1) * FOLD, :], op=op
+                    )
+
+            def finish(part):
+                here = feats(part)
+                there = slice(here.start // 4, here.stop // 4)
                 half = FOLD // 2
                 while half >= 1:
                     for tree, op in trees:
                         nc.vector.tensor_tensor(
-                            out=tree[:, 0:half, :], in0=tree[:, 0:half, :], in1=tree[:, half : 2 * half, :], op=op
+                            out=tree[:, 0:half, here], in0=tree[:, 0:half, here], in1=tree[:, half : 2 * half, here], op=op
                         )
                     half //= 2
-                ends = work.tile([P, 2, 4, PEAK_PART], F32, tag="terms", bufs=TERM_BUFS)
+                ends = work.tile([P, 2, 4, P], F32, tag="terms", bufs=TERM_BUFS)
                 for i, (tree, op) in enumerate(trees):
                     nc.vector.scalar_tensor_tensor(
-                        out=ends[:, i, :, :], in0=lin_chunks(g)[:, :, there], scalar=-1.0,
-                        in1=tree[:, 0, :].rearrange("b (p t) -> b t p", t=4), op0=ALU.mult, op1=ALU.mult,
+                        out=ends[:, i, :, there], in0=lin_chunks(g)[:, :, there], scalar=-1.0,
+                        in1=tree[:, 0, here].rearrange("b (p t) -> b t p", t=4), op0=ALU.mult, op1=ALU.mult,
                     )
                 nc.vector.tensor_tensor(
-                    out=neg_peaks[g][:, :, there], in0=ends[:, 0, :, :], in1=ends[:, 1, :, :], op=ALU.min
+                    out=neg_peaks[g][:, :, there], in0=ends[:, 0, :, there], in1=ends[:, 1, :, there], op=ALU.min
                 )
 
-            return [(fold, (i,)) for i in range(1, S // FOLD)] + [(finish, ())]
+            return fold, finish
 
         def chunk_of(g, t):
             return enc_passes[g][:].rearrange("b s (p t) -> b s t p", t=4)[:, :, t, :]
@@ -364,22 +372,25 @@ def tile_decoderlstm_pa_kernel(
                 )
             if row + ACTS_A_STEP < SCALAR_PART:
                 return
-            cols = slice(half * SCALAR_PART, (half + 1) * SCALAR_PART)
             for part in range(HALVES):
-                steps = slice(part * S_HALF, (part + 1) * S_HALF)
-                if half == 0:
-                    terms = work.tile([P, S_HALF, P], F32, tag="terms", bufs=TERM_BUFS)
-                    chunk[c, "terms"].append(terms)
-                nc.vector.tensor_tensor(
-                    out=chunk[c, "terms"][part][:, :, cols].rearrange("b (h l) p -> b h p l", l=2),
-                    in0=exps[:, :, steps].rearrange("b p (h l) -> b h p l", l=2),
-                    in1=chunk_of(g, t)[:, steps, cols].rearrange("b (h l) p -> b h p l", l=2),
-                    op=ALU.mult,
-                )
+                later(TERM_LAG + part, scalar_terms, c, half, part, exps)
+            if half == 1:
+                later(TURN_LAG, turn_exp_sum, c)
+                later(TERM_LAG + SUM_LAG, sum_scalar_chunk, c)
+
+        def scalar_terms(c, half, part, exps):
+            g, t = divmod(c, 4)
+            cols = slice(half * SCALAR_PART, (half + 1) * SCALAR_PART)
+            steps = slice(part * S_HALF, (part + 1) * S_HALF)
             if half == 0:
-                return
-            later(1, turn_exp_sum, c)
-            later(SUM_LAG, sum_scalar_chunk, c)
+                terms = work.tile([P, S_HALF, P], F32, tag="terms", bufs=TERM_BUFS)
+                chunk[c, "terms"].append(terms)
+            nc.vector.tensor_tensor(
+                out=chunk[c, "terms"][part][:, :, cols].rearrange("b (h l) p -> b h p l", l=2),
+                in0=exps[:, :, steps].rearrange("b p (h l) -> b h p l", l=2),
+                in1=chunk_of(g, t)[:, steps, cols].rearrange("b (h l) p -> b h p l", l=2),
+                op=ALU.mult,
+            )
 
         def turn_exp_sum(c):
             exp_total = psum.tile([P, P], F32, tag="sums", bufs=SUM_BANKS)
@@ -492,7 +503,10 @@ def tile_decoderlstm_pa_kernel(
                 run_waiting(now["half passes"])
 
         neg_peaks = [work.tile([P, 4, P], F32, tag="neg_peak", name="neg_peak") for g in range(H_PASSES)]
-        peak_steps = negated_peaks(0, 0) + negated_peaks(0, 1)
+        fold, finish = negated_peaks(0)
+        peak_steps = []
+        for part in range(2):
+            peak_steps.extend([(fold, (i, part)) for i in range(1, S // FOLD)] + [(finish, (part,))])
         peaks_taken = []
 
         def first_peak_steps(n):
@@ -500,14 +514,11 @@ def tile_decoderlstm_pa_kernel(
                 step(*args)
                 peaks_taken.append(step)
 
-        def run_both(first, second):
-            for step, args in (first, second):
-                step(*args)
-
         vector_stream = []
         for c in VECTOR_CHUNKS:
             if c == VECTOR_CHUNKS[1]:
-                vector_stream.extend([(run_both, pair) for pair in zip(negated_peaks(1, 0), negated_peaks(1, 1))])
+                fold, finish = negated_peaks(1)
+                vector_stream.extend([(fold, (i, None)) for i in range(1, S // FOLD)] + [(finish, (None,))])
             for step in (vector_scores, vector_exps):
                 vector_stream.extend([(step, (c, part)) for part in range(HALVES)])
         half_passes = []

@@ -36,6 +36,8 @@ VECTOR_CHUNKS = (2, 4, 6)
 SCALAR_CHUNKS = (0, 1, 3, 5, 7)
 ACTS_A_STEP = 8
 SCALAR_START = 4
+FOLDS_FIRST = 5
+QUARTERS_FIRST = 2
 FIRST_ACTS = 6
 FIRST_PEAKS = 4
 FOLDS_BEHIND = 3
@@ -43,6 +45,7 @@ PEAKS_END = 6
 SCALAR_END = 86
 VECTOR_END = 78
 CELL_START = 92
+VECTOR_COPIES = 12
 ACT_LAG = 1
 QUANTISE_LAG = 2
 MULTIPLY_LAG = 3
@@ -77,7 +80,7 @@ def new_weight_operand(stage):
     return codes[:], plane[:]
 
 
-def transpose_half(nc, psum, ident, words, pair, grouped):
+def transpose_half(nc, psum, ident, words, pair, grouped, by_vector=False):
     bank = psum.tile([P, 2, 2 * P], F32, tag="wt", bufs=TURN_BANKS)
     for i in range(2):
         for u in range(2):
@@ -85,9 +88,11 @@ def transpose_half(nc, psum, ident, words, pair, grouped):
                 bank[:, u, i * P : (i + 1) * P], words[:, 2 * pair + i, u : PASS_WORDS : 2], ident[:]
             )
     grouped_words = grouped[:].bitcast(F32).rearrange("p (r u) -> p r u", u=2)
-    nc.scalar.copy(
-        out=grouped_words[:, pair * 2 * P : (pair + 1) * 2 * P, :], in_=bank[:].rearrange("p u r -> p r u")
-    )
+    out, in_ = grouped_words[:, pair * 2 * P : (pair + 1) * 2 * P, :], bank[:].rearrange("p u r -> p r u")
+    if by_vector:
+        nc.vector.tensor_copy(out=out, in_=in_)
+    else:
+        nc.scalar.copy(out=out, in_=in_)
 
 
 def multiply(nc, acc, passes, start=True, stop=True):
@@ -157,8 +162,9 @@ def tile_decoderlstm_pa_kernel(
         enc_passes = []
         x_sb = stage.tile([P, H], BF16, tag="grouped", bufs=3, align_bytes=64)
         nc.sync.dma_start(out=x_sb[:], in_=x)
-        load_enc_steps(0, range(4), 0)
+        load_enc_steps(0, range(QUARTERS_FIRST), 0)
         attn_words = load_attn_rows(0)
+        load_enc_steps(0, range(QUARTERS_FIRST, 4), 0)
         attn_b_all = stage.tile([P, H], BF16, tag="attn_b", bufs=1)
         nc.sync.dma_start(out=attn_b_all[:], in_=attn_b.partition_broadcast(P))
 
@@ -223,7 +229,8 @@ def tile_decoderlstm_pa_kernel(
             if pair == 0:
                 now["grouped"] = new_grouped(stage)
             transpose_half(
-                nc, psum, ident, now["words"][kind][:, :, g * PASS_WORDS : (g + 1) * PASS_WORDS], pair, now["grouped"]
+                nc, psum, ident, now["words"][kind][:, :, g * PASS_WORDS : (g + 1) * PASS_WORDS], pair, now["grouped"],
+                by_vector=now["half passes"] % VECTOR_COPIES == VECTOR_COPIES - 1,
             )
             if pair == 1:
                 later(QUANTISE_LAG, quantise_pass, nb, kind, g, now["grouped"])
@@ -546,7 +553,7 @@ def tile_decoderlstm_pa_kernel(
             load_enc_steps(0, range(4), 1)
             first_peak_steps(1)
             quantise_activations(nc, x_turned, x_codes, x_planes)
-            first_peak_steps(S // FOLD - 2)
+            first_peak_steps(FOLDS_FIRST - 1)
             passes = []
             for g in range(H_PASSES):
                 grouped = new_grouped(stage)
@@ -555,16 +562,19 @@ def tile_decoderlstm_pa_kernel(
                 codes, plane = new_weight_operand(stage)
                 nc.vector.quantize_mx(out=codes.bitcast(FP8X4), scales=plane, in_=grouped[:])
                 passes.append((x_codes[:, g, :], x_planes[:, g, :], codes, plane))
-            h_turned = turn_activations(nc, psum, stage, ident, h_sb)
+            first_peak_steps(S // FOLD - 1 - FOLDS_FIRST)
             acc = psum.tile([P, N_BLOCK], F32, tag="acc", bufs=ACC_BANKS)
             multiply(nc, acc, passes)
             add_attn_bias(0, acc)
             first_peak_steps(1)
+            now["half passes"] = 0
+            for step, args in scalar_stream[: FIRST_ACTS // 2]:
+                step(*args)
+            h_turned = turn_activations(nc, psum, stage, ident, h_sb)
+            for step, args in scalar_stream[FIRST_ACTS // 2 : FIRST_ACTS]:
+                step(*args)
             first_peak_steps(FOLDS_BEHIND)
             quantise_activations(nc, h_turned, h_codes, h_planes)
-            now["half passes"] = 0
-            for step, args in scalar_stream[:FIRST_ACTS]:
-                step(*args)
             first_peak_steps(FIRST_PEAKS)
             merge(
                 (

from contextlib import ExitStack

import concourse.mybir as mybir
from concourse.masks import make_identity

F32 = mybir.dt.float32
BF16 = mybir.dt.bfloat16
U32 = mybir.dt.uint32
U8 = mybir.dt.uint8
FP8X4 = mybir.dt.float8_e4m3fn_x4
ALU = mybir.AluOpType
ACT = mybir.ActivationFunctionType

P = 128
H = 1024
S = 32
K_PASS = 512
PASS_WORDS = K_PASS // 2
H_PASSES = H // K_PASS
N_BLOCK = 512
ROW_TILES = N_BLOCK // P
H_BLOCKS = H // N_BLOCK
GATE_BLOCKS = 4 * H_BLOCKS
LATE_BLOCK = 7
EARLY_BLOCKS = 4
ATTN = -1
ENC_LOADS = {0: range(0, 1), 1: range(1, 4)}
TERM_BUFS = 4
CODE_BUFS = 5
ACC_BANKS = 1
TURN_BANKS = 4
SUM_BANKS = 3
CHUNKS = 8
SCALAR_PART = P // 2
VECTOR_CHUNKS = (2, 4, 6)
SCALAR_CHUNKS = (0, 1, 3, 5, 7)
ACTS_A_STEP = 8
SCALAR_START = 4
FOLDS_FIRST = 5
QUARTERS_FIRST = 2
FIRST_ACTS = 6
FIRST_PEAKS = 4
FOLDS_BEHIND = 3
PEAKS_END = 6
SCALAR_END = 86
VECTOR_END = 78
CELL_START = 92
VECTOR_COPIES = 12
ACT_LAG = 1
QUANTISE_LAG = 2
MULTIPLY_LAG = 3
SUM_PIECE = 8
TURN_LAG = 2
TERM_LAG = 1
SUM_LAG = 3
EXP_LAG = 3
QUARTER = S // 4
PEAK_PART = P // 2
FOLD = 4
S_HALF = S // 2
HALVES = S // S_HALF

FLOPS = 2 * P * (H * H + 4 * H * 3 * H)


def load_weight_rows(nc, stage, rows, order="(t p) k -> p t k"):
    w_rows = stage.tile([P, ROW_TILES, H], BF16, tag="w_rows", bufs=3)
    nc.sync.dma_start(out=w_rows[:], in_=rows.rearrange(order, p=P))
    return w_rows[:].bitcast(F32)


def new_grouped(stage):
    grouped = stage.tile([P, 4 * N_BLOCK], BF16, tag="grouped", bufs=3, align_bytes=64)
    return grouped


def new_weight_operand(stage):
    codes = stage.tile([P, N_BLOCK], U32, tag="w_codes", bufs=CODE_BUFS, align_bytes=64)
    plane = stage.tile([P, N_BLOCK], U8, tag="w_plane", bufs=CODE_BUFS, align_bytes=64)
    return codes[:], plane[:]


def transpose_half(nc, psum, ident, words, pair, grouped, by_vector=False):
    bank = psum.tile([P, 2, 2 * P], F32, tag="wt", bufs=TURN_BANKS)
    for i in range(2):
        for u in range(2):
            nc.tensor.transpose(
                bank[:, u, i * P : (i + 1) * P], words[:, 2 * pair + i, u : PASS_WORDS : 2], ident[:]
            )
    grouped_words = grouped[:].bitcast(F32).rearrange("p (r u) -> p r u", u=2)
    out, in_ = grouped_words[:, pair * 2 * P : (pair + 1) * 2 * P, :], bank[:].rearrange("p u r -> p r u")
    if by_vector:
        nc.vector.tensor_copy(out=out, in_=in_)
    else:
        nc.scalar.copy(out=out, in_=in_)


def multiply(nc, acc, passes, start=True, stop=True):
    for i, (a_codes, a_plane, w_codes, w_plane) in enumerate(passes):
        nc.tensor.matmul_mx(
            out=acc[:],
            lhsT=a_codes.bitcast(FP8X4),
            lhsT_scale=a_plane,
            rhs=w_codes.bitcast(FP8X4),
            rhs_scale=w_plane,
            start=(start and i == 0),
            stop=(stop and i == len(passes) - 1),
        )


def turn_activations(nc, psum, stage, ident, rows):
    words = rows[:].bitcast(F32)
    bank = psum.tile([P, 2 * H_PASSES, P], F32, tag="wt", bufs=TURN_BANKS)
    for q in range(2 * H_PASSES):
        nc.tensor.transpose(
            bank[:, q, :], words[:, (q // 2) * PASS_WORDS + q % 2 : (q // 2 + 1) * PASS_WORDS : 2], ident[:]
        )
    grouped = stage.tile([P, 4 * H_PASSES * P], BF16, tag="grouped", bufs=3, align_bytes=64)
    nc.scalar.copy(
        out=grouped[:].bitcast(F32).rearrange("p (g b u) -> p g b u", g=H_PASSES, u=2),
        in_=bank[:].rearrange("p (g u) b -> p g b u", u=2),
    )
    return grouped


def quantise_activations(nc, grouped, codes, planes):
    nc.vector.quantize_mx(
        out=codes[:].rearrange("p g b -> p (g b)").bitcast(FP8X4),
        scales=planes[:].rearrange("p g b -> p (g b)"),
        in_=grouped[:],
    )


def tile_decoderlstm_pa_kernel(
    tc, x, enc_seq, attn_W, attn_b, h_prev, c_prev, W_ih0, W_hh0, b_ih0, b_hh0, out_0, out_1
):
    nc = tc.nc
    with ExitStack() as stack:
        const = stack.enter_context(tc.tile_pool(name="const", bufs=1))
        keep = stack.enter_context(tc.tile_pool(name="keep", bufs=1))
        stage = stack.enter_context(tc.tile_pool(name="stage", bufs=2))
        work = stack.enter_context(tc.tile_pool(name="work", bufs=2))
        psum = stack.enter_context(tc.psum_pool(name="psum", bufs=2))

        def load_enc_steps(g, quarters, part=None):
            if len(enc_passes) == g:
                enc_passes.append(work.tile([P, S, K_PASS], BF16, tag="enc", name="enc", align_bytes=64))
            here = slice(0, K_PASS) if part is None else slice(4 * part * PEAK_PART, 4 * (part + 1) * PEAK_PART)
            feats = slice(g * K_PASS + here.start, g * K_PASS + here.stop)
            for i in quarters:
                steps = slice(i * QUARTER, (i + 1) * QUARTER)
                nc.sync.dma_start(out=enc_passes[g][:, steps, here], in_=enc_seq[steps, :, feats].rearrange("s b j -> b s j"))

        def load_attn_rows(nb):
            return load_weight_rows(nc, stage, attn_W[nb * N_BLOCK : (nb + 1) * N_BLOCK, :], "(p t) k -> p t k")

        ident = const.tile([P, P], F32)
        make_identity(nc, ident[:])
        warm_exp = const.tile([P, 1], F32)
        nc.scalar.activation(out=warm_exp[:], in_=ident[:, 0:1], func=ACT.Exp)

        enc_passes = []
        x_sb = stage.tile([P, H], BF16, tag="grouped", bufs=3, align_bytes=64)
        nc.sync.dma_start(out=x_sb[:], in_=x)
        load_enc_steps(0, range(QUARTERS_FIRST), 0)
        attn_words = load_attn_rows(0)
        load_enc_steps(0, range(QUARTERS_FIRST, 4), 0)
        attn_b_all = stage.tile([P, H], BF16, tag="attn_b", bufs=1)
        nc.sync.dma_start(out=attn_b_all[:], in_=attn_b.partition_broadcast(P))

        biases = [work.tile([P, 4 * H // P], BF16, tag="bias", name="bias") for i in range(2)]
        for bias, b_hbm in zip(biases, (b_ih0, b_hh0)):
            nc.gpsimd.dma_start(out=bias[:], in_=b_hbm.rearrange("(p n) -> p n", p=P))
        bias_sum = work.tile([P, 4 * H // P], F32, tag="bias_sum", bufs=1)
        nc.gpsimd.tensor_tensor(out=bias_sum[:], in0=biases[0][:], in1=biases[1][:], op=ALU.add)
        parked = out_0[0:4, :].rearrange("r n -> (r n)")
        nc.gpsimd.dma_start(out=parked.rearrange("(p n) -> p n", p=P), in_=bias_sum[:])
        gates_xh = keep.tile([P, 4 * H], F32)

        x_codes = keep.tile([P, H_PASSES, P], U32, align_bytes=64)
        x_planes = keep.tile([P, H_PASSES, P], U8, align_bytes=64)
        h_codes = keep.tile([P, H_PASSES, P], U32, align_bytes=64)
        h_planes = keep.tile([P, H_PASSES, P], U8, align_bytes=64)

        attn_lin = keep.tile([P, H], F32)

        def add_attn_bias(nb, acc):
            cols = slice(nb * N_BLOCK, (nb + 1) * N_BLOCK)
            nc.vector.tensor_tensor(
                out=attn_lin[:, cols].rearrange("b (t p) -> b t p", p=P),
                in0=acc[:].rearrange("b (t p) -> b t p", p=P),
                in1=attn_b_all[:, cols].rearrange("b (p t) -> b t p", p=P),
                op=ALU.add,
            )

        def load_c():
            c_sb = work.tile([P, H], BF16, tag="exps_v", bufs=2)
            nc.sync.dma_start(out=c_sb[:], in_=c_prev)
            now["c"] = c_sb

        wa_codes = [keep.tile([P, EARLY_BLOCKS, H_PASSES, N_BLOCK], U32, align_bytes=64, name="wa_codes")]
        wa_planes = keep.tile([P, GATE_BLOCKS // 2, N_BLOCK], U8, align_bytes=64)

        def wa_code(nb, g):
            late, at = divmod(nb, EARLY_BLOCKS)
            return wa_codes[late][:, at, g, :]

        def wa_plane(nb, g):
            row = 4 * (2 * (nb % 2) + g)
            return wa_planes[row:P, nb // 2, :]

        att_codes = keep.tile([P, H_PASSES, P], U32, align_bytes=64)
        att_planes = keep.tile([P, H_PASSES, P], U8, align_bytes=64)

        def load_gate_block(nb):
            rows = slice(nb * N_BLOCK, (nb + 1) * N_BLOCK)
            return [load_weight_rows(nc, stage, w) for w in (W_ih0[rows, 0:H], W_hh0[rows, :], W_ih0[rows, H : 2 * H])]

        now = {"passes": []}
        waiting = []

        def weight_step(nb, kind, g, pair):
            if (kind, g, pair) == (0, 0, 0):
                now["words"] = [load_attn_rows(1)] if nb == ATTN else load_gate_block(nb)
                if nb == 0:
                    nc.sync.dma_start(out=gates_xh[:], in_=parked.partition_broadcast(P))
                if nb in ENC_LOADS:
                    load_enc_steps(1, ENC_LOADS[nb])
            if pair == 0:
                now["grouped"] = new_grouped(stage)
            transpose_half(
                nc, psum, ident, now["words"][kind][:, :, g * PASS_WORDS : (g + 1) * PASS_WORDS], pair, now["grouped"],
                by_vector=now["half passes"] % VECTOR_COPIES == VECTOR_COPIES - 1,
            )
            if pair == 1:
                later(QUANTISE_LAG, quantise_pass, nb, kind, g, now["grouped"])

        def quantise_pass(nb, kind, g, grouped):
            act_codes, act_planes = ((x_codes, x_planes), (h_codes, h_planes), (att_codes, att_planes))[kind]
            kept = kind == 2 and nb < LATE_BLOCK
            if kept:
                if nb == EARLY_BLOCKS and g == 0:
                    wa_codes.append(
                        work.tile([P, LATE_BLOCK - EARLY_BLOCKS, H_PASSES, N_BLOCK], U32, tag="enc", name="wa_codes", align_bytes=64)
                    )
                codes, plane = wa_code(nb, g), wa_plane(nb, g)
            else:
                codes, plane = new_weight_operand(stage)
            nc.vector.quantize_mx(out=codes.bitcast(FP8X4), scales=plane, in_=grouped[:])
            if kept:
                return
            now["passes"].append((act_codes[:, g, :], act_planes[:, g, :], codes, plane))
            if (kind, g) in ((2, 1), (0 if nb == ATTN else 1, 1)):
                later(MULTIPLY_LAG, add_products, nb, kind, now["passes"])
                now["passes"] = []

        def add_products(nb, kind, passes):
            if kind < 2:
                acc = psum.tile([P, N_BLOCK], F32, tag="acc", bufs=ACC_BANKS)
                now["acc"] = acc
            last = kind == 2 or nb < LATE_BLOCK
            multiply(nc, now["acc"], passes, start=(kind < 2), stop=last)
            if last and nb == ATTN:
                add_attn_bias(1, now["acc"])
            elif last and nb >= LATE_BLOCK:
                add_and_activate(nb % H_BLOCKS, 3, now["acc"])
            elif last:
                rows = slice(nb * N_BLOCK, (nb + 1) * N_BLOCK)
                nc.vector.tensor_tensor(out=gates_xh[:, rows], in0=now["acc"][:], in1=gates_xh[:, rows], op=ALU.add)

        def lin_chunks(g):
            return attn_lin[:, g * K_PASS : (g + 1) * K_PASS].rearrange("b (t p) -> b t p", p=P)

        def negated_peaks(g):
            trees = []

            def feats(part):
                return slice(0, K_PASS) if part is None else slice(4 * part * PEAK_PART, 4 * (part + 1) * PEAK_PART)

            def fold(i, part):
                if not trees:
                    top = work.tile([P, FOLD, K_PASS], BF16, tag="top", bufs=1)
                    low = work.tile([P, FOLD, K_PASS], BF16, tag="low", bufs=1)
                    trees.extend([(top, ALU.max), (low, ALU.min)])
                here = feats(part)
                enc = enc_passes[g][:, :, here]
                for tree, op in trees:
                    before = enc[:, 0:FOLD, :] if i == 1 else tree[:, :, here]
                    nc.vector.tensor_tensor(
                        out=tree[:, :, here], in0=before, in1=enc[:, i * FOLD : (i + 1) * FOLD, :], op=op
                    )

            def finish(part):
                here = feats(part)
                there = slice(here.start // 4, here.stop // 4)
                half = FOLD // 2
                while half >= 1:
                    for tree, op in trees:
                        nc.vector.tensor_tensor(
                            out=tree[:, 0:half, here], in0=tree[:, 0:half, here], in1=tree[:, half : 2 * half, here], op=op
                        )
                    half //= 2
                ends = work.tile([P, 2, 4, P], F32, tag="terms", bufs=TERM_BUFS)
                for i, (tree, op) in enumerate(trees):
                    nc.vector.scalar_tensor_tensor(
                        out=ends[:, i, :, there], in0=lin_chunks(g)[:, :, there], scalar=-1.0,
                        in1=tree[:, 0, here].rearrange("b (p t) -> b t p", t=4), op0=ALU.mult, op1=ALU.mult,
                    )
                nc.vector.tensor_tensor(
                    out=neg_peaks[g][:, :, there], in0=ends[:, 0, :, there], in1=ends[:, 1, :, there], op=ALU.min
                )

            return fold, finish

        def chunk_of(g, t):
            return enc_passes[g][:].rearrange("b s (p t) -> b s t p", t=4)[:, :, t, :]

        def add_positions(c, name, tiles, part, first, behind):
            if part == 0 and first == 0:
                total = psum.tile([P, P], F32, tag="sums", bufs=SUM_BANKS)
                chunk[c, name] = total
            for i in range(first, first + SUM_PIECE):
                s = part * S_HALF + i
                nc.tensor.matmul(
                    out=chunk[c, name][:], lhsT=tiles[:, i, :], rhs=ident[:], is_transpose=True,
                    start=(s == 0), stop=(s == S - 1),
                )
            if first + SUM_PIECE < S_HALF:
                later(1, add_positions, c, name, tiles, part, first + SUM_PIECE, behind)
            elif behind:
                step, args = behind
                step(*args)

        att_t = [work.tile([P, 4, P], F32, tag="att_t", name="att_t") for g in range(H_PASSES)]
        chunks_left = [4] * H_PASSES
        chunk = {}

        def finish_chunk(c):
            g, t = divmod(c, 4)
            nc.vector.tensor_tensor(out=att_t[g][:, t, :], in0=chunk[c, "total"][:], in1=chunk[c, "inverse"][:], op=ALU.mult)
            chunks_left[g] -= 1
            if chunks_left[g] == 0:
                att_grouped = stage.tile([P, P, 4], BF16, tag="grouped", bufs=3, align_bytes=64)
                nc.vector.tensor_copy(out=att_grouped[:], in_=att_t[g][:].rearrange("p t b -> p b t"))
                nc.vector.quantize_mx(
                    out=att_codes[:, g, :].bitcast(FP8X4),
                    scales=att_planes[:, g, :],
                    in_=att_grouped[:].rearrange("p b t -> p (b t)"),
                )

        def invert_sum(c):
            exp_total = chunk[c, "exp_total"]
            inverse = work.tile([P, P], F32, tag="inverse")
            nc.vector.reciprocal(out=inverse[:], in_=exp_total[:])
            chunk[c, "inverse"] = inverse

        def scalar_step(step):
            at, i = divmod(step, P // ACTS_A_STEP)
            c = SCALAR_CHUNKS[at]
            g, t = divmod(c, 4)
            half, row = divmod(i * ACTS_A_STEP, SCALAR_PART)
            if i == 0:
                exp_sum = work.tile([P, P], F32, tag="exp_sum")
                chunk[c, "exp_sum"] = exp_sum
                chunk[c, "terms"] = []
            if row == 0:
                exps = work.tile([P, SCALAR_PART, S], F32, tag="exps_s", bufs=2)
                chunk[c, "exps"] = exps
            exps, exp_sum = chunk[c, "exps"], chunk[c, "exp_sum"]
            for k in range(row, row + ACTS_A_STEP):
                p = half * SCALAR_PART + k
                nc.scalar.activation(
                    out=exps[:, k, :],
                    in_=enc_passes[g][:, :, 4 * p + t],
                    func=ACT.Exp,
                    scale=lin_chunks(g)[:, t, p : p + 1],
                    bias=neg_peaks[g][:, t, p : p + 1],
                    accum_out=exp_sum[:, p : p + 1],
                )
            if row + ACTS_A_STEP < SCALAR_PART:
                return
            for part in range(HALVES):
                later(TERM_LAG + part, scalar_terms, c, half, part, exps)
            if half == 1:
                later(TURN_LAG, turn_exp_sum, c)
                later(TERM_LAG + SUM_LAG, sum_scalar_chunk, c)

        def scalar_terms(c, half, part, exps):
            g, t = divmod(c, 4)
            cols = slice(half * SCALAR_PART, (half + 1) * SCALAR_PART)
            steps = slice(part * S_HALF, (part + 1) * S_HALF)
            if half == 0:
                terms = work.tile([P, S_HALF, P], F32, tag="terms", bufs=TERM_BUFS)
                chunk[c, "terms"].append(terms)
            nc.vector.tensor_tensor(
                out=chunk[c, "terms"][part][:, :, cols].rearrange("b (h l) p -> b h p l", l=2),
                in0=exps[:, :, steps].rearrange("b p (h l) -> b h p l", l=2),
                in1=chunk_of(g, t)[:, steps, cols].rearrange("b (h l) p -> b h p l", l=2),
                op=ALU.mult,
            )

        def turn_exp_sum(c):
            exp_total = psum.tile([P, P], F32, tag="sums", bufs=SUM_BANKS)
            nc.tensor.transpose(exp_total[:], chunk[c, "exp_sum"][:], ident[:])
            chunk[c, "exp_total"] = exp_total
            invert_sum(c)

        def sum_scalar_chunk(c):
            terms = chunk[c, "terms"]
            second = (add_positions, (c, "total", terms[1], 1, 0, (finish_chunk, (c,))))
            add_positions(c, "total", terms[0], 0, 0, (later, (1,) + second[:1] + second[1]))

        def vector_scores(c, part):
            g, t = divmod(c, 4)
            exps = work.tile([P, S_HALF, P], F32, tag="exps_v", bufs=2)
            nc.vector.tensor_tensor(
                out=exps[:], in0=chunk_of(g, t)[:, part * S_HALF : (part + 1) * S_HALF, :],
                in1=lin_chunks(g)[:, t, :].unsqueeze(1).to_broadcast([P, S_HALF, P]), op=ALU.mult,
            )
            chunk[c, part] = exps

        def vector_exps(c, part):
            g, t = divmod(c, 4)
            exps = chunk[c, part]
            nc.vector.tensor_tensor(
                out=exps[:], in0=exps[:],
                in1=neg_peaks[g][:, t, :].unsqueeze(1).to_broadcast([P, S_HALF, P]), op=ALU.add,
            )
            later(EXP_LAG, exp_vector_scores, c, part)

        def exp_vector_scores(c, part):
            exps = chunk[c, part]
            nc.scalar.activation(out=exps[:], in_=exps[:], func=ACT.Exp)
            later(EXP_LAG, sum_vector_exps, c, part)

        def sum_vector_exps(c, part):
            behind = (invert_sum, (c,)) if part == HALVES - 1 else None
            add_positions(c, "exp_total", chunk[c, part], part, 0, behind)
            vector_terms(c, part)

        def vector_terms(c, part):
            g, t = divmod(c, 4)
            terms = work.tile([P, S_HALF, P], F32, tag="terms", bufs=TERM_BUFS)
            nc.vector.tensor_tensor(
                out=terms[:], in0=chunk[c, part][:], in1=chunk_of(g, t)[:, part * S_HALF : (part + 1) * S_HALF, :], op=ALU.mult
            )
            chunk[c, "terms", part] = terms
            later(SUM_LAG, sum_vector_terms, c, part)

        def sum_vector_terms(c, part):
            behind = (finish_chunk, (c,)) if part == HALVES - 1 else None
            add_positions(c, "total", chunk[c, "terms", part], part, 0, behind)

        def add_and_activate(part, i, acc):
            value = cells[0][:, part, i, :]
            nb = i * H_BLOCKS + part
            nc.vector.tensor_tensor(out=value, in0=acc[:], in1=gates_xh[:, nb * N_BLOCK : (nb + 1) * N_BLOCK], op=ALU.add)
            later(ACT_LAG, activate, value, ACT.Tanh if i == 2 else ACT.Sigmoid)

        def activate(value, func):
            nc.scalar.activation(out=value, in_=value, func=func)

        def gate(part, i):
            nb = i * H_BLOCKS + part
            acc = psum.tile([P, N_BLOCK], F32, tag="sums", bufs=SUM_BANKS)
            multiply(nc, acc, [(att_codes[:, g, :], att_planes[:, g, :], wa_code(nb, g), wa_plane(nb, g)) for g in range(H_PASSES)])
            add_and_activate(part, i, acc)

        def new_cell_state(part):
            cols = slice(part * N_BLOCK, (part + 1) * N_BLOCK)
            gate_i, gate_f, gate_g = [cells[0][:, part, i, :] for i in range(3)]
            kept, c_new, tanh_c = [cells[0][:, part, i, :] for i in range(4, 7)]
            nc.vector.tensor_tensor(out=kept, in0=gate_f, in1=now["c"][:, cols], op=ALU.mult)
            nc.vector.tensor_tensor(out=c_new, in0=gate_i, in1=gate_g, op=ALU.mult)
            nc.vector.tensor_tensor(out=c_new, in0=c_new, in1=kept, op=ALU.add)
            nc.sync.dma_start(out=out_1[:, cols], in_=c_new)
            later(ACT_LAG, activate_into, tanh_c, c_new)

        def activate_into(tanh_c, c_new):
            nc.scalar.activation(out=tanh_c, in_=c_new, func=ACT.Tanh)

        def new_hidden_state(part):
            h_new = cells[0][:, part, 7, :]
            nc.vector.tensor_tensor(out=h_new, in0=cells[0][:, part, 3, :], in1=cells[0][:, part, 6, :], op=ALU.mult)
            nc.sync.dma_start(out=out_0[:, part * N_BLOCK : (part + 1) * N_BLOCK], in_=h_new)

        def later(lag, step, *args):
            waiting.append((now["half passes"] + lag, step, args))

        def run_waiting(upto):
            due = [entry for entry in waiting if entry[0] <= upto]
            for entry in due:
                waiting.remove(entry)
            for at, step, args in due:
                step(*args)

        def merge(streams):
            taken = [0] * len(streams)
            for w, half_pass in enumerate(half_passes):
                now["half passes"] = w
                run_waiting(w)
                for i, (first, last, steps) in enumerate(streams):
                    upto = min(len(steps), max(0, -(-(w + 1 - first) * len(steps) // (last - first))))
                    for step, args in steps[taken[i] : upto]:
                        step(*args)
                    taken[i] = upto
                weight_step(*half_pass)
            while waiting:
                now["half passes"] = min(entry[0] for entry in waiting)
                run_waiting(now["half passes"])

        neg_peaks = [work.tile([P, 4, P], F32, tag="neg_peak", name="neg_peak") for g in range(H_PASSES)]
        fold, finish = negated_peaks(0)
        peak_steps = []
        for part in range(2):
            peak_steps.extend([(fold, (i, part)) for i in range(1, S // FOLD)] + [(finish, (part,))])
        peaks_taken = []

        def first_peak_steps(n):
            for step, args in peak_steps[len(peaks_taken) : len(peaks_taken) + n]:
                step(*args)
                peaks_taken.append(step)

        vector_stream = []
        for c in VECTOR_CHUNKS:
            if c == VECTOR_CHUNKS[1]:
                fold, finish = negated_peaks(1)
                vector_stream.extend([(fold, (i, None)) for i in range(1, S // FOLD)] + [(finish, (None,))])
            for step in (vector_scores, vector_exps):
                vector_stream.extend([(step, (c, part)) for part in range(HALVES)])
        half_passes = []
        for nb in range(GATE_BLOCKS):
            if nb == 1:
                half_passes.extend([(ATTN, 0, g, pair) for g in range(H_PASSES) for pair in range(2)])
            half_passes.extend([(nb, kind, g, pair) for kind in range(3) for g in range(H_PASSES) for pair in range(2)])
        scalar_stream = [(scalar_step, (i,)) for i in range(len(SCALAR_CHUNKS) * P // ACTS_A_STEP)]

        def start_cell():
            warm = work.tile([P, 1], F32, tag="warm", bufs=1)
            nc.scalar.activation(out=warm[:], in_=ident[:, 0:1], func=ACT.Sigmoid)
            cells.append(work.tile([P, H_BLOCKS, 8, N_BLOCK], F32, tag="enc", name="cells", align_bytes=64))

        cells = []
        cell_stream = [(load_c, ()), (start_cell, ())]
        for part in range(H_BLOCKS):
            cell_stream.extend([(gate, (part, i)) for i in range(4) if i * H_BLOCKS + part < LATE_BLOCK])
            cell_stream.append((later, (ACT_LAG, new_cell_state, part)))
        cell_stream.extend([(later, (2 * ACT_LAG + 1, new_hidden_state, part)) for part in range(H_BLOCKS - 1)])
        with tc.manual_schedule(engines={mybir.EngineType.Activation, mybir.EngineType.PE, mybir.EngineType.DVE}):
            x_turned = turn_activations(nc, psum, stage, ident, x_sb)
            h_sb = stage.tile([P, H], BF16, tag="grouped", bufs=3, align_bytes=64)
            nc.sync.dma_start(out=h_sb[:], in_=h_prev)
            load_enc_steps(0, range(4), 1)
            first_peak_steps(1)
            quantise_activations(nc, x_turned, x_codes, x_planes)
            first_peak_steps(FOLDS_FIRST - 1)
            passes = []
            for g in range(H_PASSES):
                grouped = new_grouped(stage)
                for pair in range(2):
                    transpose_half(nc, psum, ident, attn_words[:, :, g * PASS_WORDS : (g + 1) * PASS_WORDS], pair, grouped)
                codes, plane = new_weight_operand(stage)
                nc.vector.quantize_mx(out=codes.bitcast(FP8X4), scales=plane, in_=grouped[:])
                passes.append((x_codes[:, g, :], x_planes[:, g, :], codes, plane))
            first_peak_steps(S // FOLD - 1 - FOLDS_FIRST)
            acc = psum.tile([P, N_BLOCK], F32, tag="acc", bufs=ACC_BANKS)
            multiply(nc, acc, passes)
            add_attn_bias(0, acc)
            first_peak_steps(1)
            now["half passes"] = 0
            for step, args in scalar_stream[: FIRST_ACTS // 2]:
                step(*args)
            h_turned = turn_activations(nc, psum, stage, ident, h_sb)
            for step, args in scalar_stream[FIRST_ACTS // 2 : FIRST_ACTS]:
                step(*args)
            first_peak_steps(FOLDS_BEHIND)
            quantise_activations(nc, h_turned, h_codes, h_planes)
            first_peak_steps(FIRST_PEAKS)
            merge(
                (
                    (0, PEAKS_END, peak_steps[len(peaks_taken) :]),
                    (SCALAR_START, SCALAR_END, scalar_stream[FIRST_ACTS:]),
                    (PEAKS_END, VECTOR_END, vector_stream),
                    (CELL_START, len(half_passes), cell_stream),
                )
            )
            new_hidden_state(H_BLOCKS - 1)
